import numpy as np
import ml_dtypes


def mxq(x, axis, fmt="e4m3"):
    dtype, down = {"e4m3": (ml_dtypes.float8_e4m3fn, 7), "e5m2": (ml_dtypes.float8_e5m2, 14)}[fmt]
    v = np.moveaxis(np.asarray(x, np.float32).astype(ml_dtypes.bfloat16).astype(np.float64), axis, -1)
    blocks = v.reshape(v.shape[:-1] + (-1, 32))
    amax = np.abs(blocks).max(-1, keepdims=True)
    byte = np.maximum(np.where(amax > 0, np.frexp(amax)[1] - 1 + 127, 0) - down, 1)
    scale = np.exp2(byte - 127.0)
    codes = (blocks / scale).astype(np.float32).astype(dtype).astype(np.float64)
    return np.moveaxis((codes * scale).reshape(v.shape), -1, axis)


WIDE = False


def mx_kscale(k):
    if not WIDE:
        return np.ones(k)
    levels = np.array([10, -10, 5, -5, 0])
    a = np.random.permutation(np.resize(levels, k // 512 * 4)).reshape(k // 512, 4)
    idx = np.arange(k)
    return np.exp2(a[idx // 512, idx % 128 // 32])


BF16 = ml_dtypes.bfloat16


def bf(x):
    return np.asarray(x, np.float32).astype(BF16)


def f64(x):
    return np.asarray(x).astype(np.float64)


B, S, H, HS, D = 256, 16, 4, 128, 1024
M = H * HS
FORGET_BIAS = 1.0


def sigmoid(v):
    return 1.0 / (1.0 + np.exp(-v))


def setup_inputs():
    s, t = mx_kscale(M), mx_kscale(D)
    n = np.random.standard_normal
    return {
        'inputs': bf(n((B, D)) * t),
        'h_state': bf(n((B, S, M)) * s),
        'm_state': bf(n((B, S, M))),
        'mem_att': bf(n((B, S, M)) * 2.0),
        'W_g': bf(n((M, M)) * 0.5 / np.sqrt(M)), 'b_g': bf(n(M) * 0.5),
        'W_wf': bf(n((D, M)) / np.sqrt(D) / t[:, None]),
        'W_wi': bf(n((D, M)) / np.sqrt(D) / t[:, None]),
        'W_wo': bf(n((D, M)) / np.sqrt(D) / t[:, None]),
        'W_uf': bf(n((M, M)) / np.sqrt(M) / s[:, None]), 'b_uf': bf(n(M)),
        'W_ui': bf(n((M, M)) / np.sqrt(M) / s[:, None]), 'b_ui': bf(n(M)),
        'W_uo': bf(n((M, M)) / np.sqrt(M) / s[:, None]), 'b_uo': bf(n(M)),
    }


def reference(inputs, h_state, m_state, mem_att, W_g, b_g, W_wf, W_wi, W_wo, W_uf, b_uf, W_ui, b_ui, W_uo, b_uo):
    m = f64(m_state)
    p = f64(mem_att)
    xq = mxq(f64(inputs), 1, 'e4m3')
    hq = mxq(f64(h_state), 2, 'e4m3')
    memory_proposal = ((mxq(p, 2, 'e4m3') @ mxq(f64(W_g), 0, 'e4m3')) + f64(b_g)) + p
    forget_gate = sigmoid((hq @ mxq(f64(W_uf), 0, 'e4m3')) + f64(b_uf) + (xq @ mxq(f64(W_wf), 0, 'e4m3'))[:, None, :])
    input_gate = sigmoid((hq @ mxq(f64(W_ui), 0, 'e4m3')) + f64(b_ui) + (xq @ mxq(f64(W_wi), 0, 'e4m3'))[:, None, :])
    output_gate = sigmoid((hq @ mxq(f64(W_uo), 0, 'e4m3')) + f64(b_uo) + (xq @ mxq(f64(W_wo), 0, 'e4m3'))[:, None, :])
    new_memories = sigmoid(m * forget_gate + FORGET_BIAS) + memory_proposal * sigmoid(input_gate)
    new_hidden = np.tanh(m) * sigmoid(output_gate)
    return new_memories, new_hidden

@@ -1,0 +1,236 @@
+from contextlib import ExitStack
+
+import concourse.mybir as mybir
+from concourse.masks import make_identity
+
+F32 = mybir.dt.float32
+BF16 = mybir.dt.bfloat16
+U32 = mybir.dt.uint32
+U8 = mybir.dt.uint8
+FP8X4 = mybir.dt.float8_e4m3fn_x4
+FUNC = mybir.ActivationFunctionType
+ALU = mybir.AluOpType
+
+P = 128
+BATCH = 256
+SLOTS = 16
+WIDTH = 512
+D_IN = 1024
+PACK = 4
+K_PASS = P * PACK
+HALVES = BATCH // P
+X_PASSES = D_IN // K_PASS
+CHUNK = 2
+
+FLOPS = 2 * (4 * BATCH * SLOTS * WIDTH * WIDTH + 3 * BATCH * D_IN * WIDTH)
+
+W_F, W_I, W_O, W_PROP = 0, 1, 2, 3
+W_X = 4
+
+
+def quantise_weight_piece(nc, stage, w_rows, words, scales):
+    raw = stage.tile([P, PACK, WIDTH], BF16, name="raw")
+    nc.sync.dma_start(
+        out=raw[:].rearrange("q (u e) n -> q u e n", u=2),
+        in_=w_rows.rearrange("(u q e) n -> q u e n", u=2, e=2),
+    )
+    grouped = stage.tile([P, WIDTH, PACK], BF16, name="grouped", align_bytes=64)
+    nc.vector.tensor_copy(
+        out=grouped[:].rearrange("q (c i) t -> q c t i", i=4),
+        in_=raw[:].rearrange("q t (c i) -> q c t i", i=4),
+    )
+    nc.vector.quantize_mx(
+        out=words.bitcast(FP8X4),
+        scales=scales,
+        in_=grouped[:].rearrange("q n t -> q (n t)"),
+    )
+
+
+def tile_relationalmemorycorecell_pa_t_kernel(
+    tc,
+    inputs,
+    h_state,
+    m_state,
+    mem_att,
+    W_g,
+    b_g,
+    W_wf,
+    W_wi,
+    W_wo,
+    W_uf,
+    b_uf,
+    W_ui,
+    b_ui,
+    W_uo,
+    b_uo,
+    out_0,
+    out_1,
+):
+    nc = tc.nc
+    with ExitStack() as pools:
+        consts = pools.enter_context(tc.tile_pool(name="consts", bufs=1))
+        stage = pools.enter_context(tc.tile_pool(name="stage", bufs=3))
+        work = pools.enter_context(tc.tile_pool(name="work", bufs=3))
+        psum_t = pools.enter_context(tc.psum_pool(name="psum_t", bufs=2))
+        psum_acc = pools.enter_context(tc.psum_pool(name="psum_acc", bufs=6))
+
+        ident = consts.tile([P, P], F32, name="ident")
+        make_identity(nc, ident[:])
+        one_col = consts.tile([P, 1], F32, name="one_col")
+        nc.vector.memset(one_col[:], 1.0)
+
+        x_words = consts.tile([P, HALVES, X_PASSES, P], U32, name="x_words", align_bytes=64)
+        x_scales = consts.tile([P, HALVES, X_PASSES, P], U8, name="x_scales", align_bytes=64)
+        for half in range(HALVES):
+            x_nat = stage.tile([P, D_IN], BF16, name="x_nat")
+            nc.sync.dma_start(out=x_nat[:], in_=inputs[half * P : (half + 1) * P, :])
+            x_pairs = x_nat[:].bitcast(F32)
+            x_t = psum_t.tile([P, X_PASSES, 2, P], F32, name="turned")
+            for g in range(X_PASSES):
+                for u in range(2):
+                    first = (2 * g + u) * P
+                    nc.tensor.transpose(x_t[:, g, u, :], x_pairs[:, first : first + P], ident[:])
+            x_grouped = stage.tile([P, X_PASSES, P, PACK], BF16, name="x_grouped", align_bytes=64)
+            nc.vector.tensor_copy(
+                out=x_grouped[:].bitcast(F32), in_=x_t[:].rearrange("q g u b -> q g b u")
+            )
+            nc.vector.quantize_mx(
+                out=x_words[:, half, :, :].rearrange("q g b -> q (g b)").bitcast(FP8X4),
+                scales=x_scales[:, half, :, :].rearrange("q g b -> q (g b)"),
+                in_=x_grouped[:].rearrange("q g b t -> q (g b t)"),
+            )
+
+        bias_rows = consts.tile([P, 4, WIDTH], BF16, name="bias_rows")
+        nc.vector.memset(bias_rows[:], 0.0)
+        for j, bias in enumerate((b_uf, b_ui, b_uo, b_g)):
+            nc.scalar.dma_start(out=bias_rows[0:1, j, :], in_=bias.unsqueeze(0))
+        ones = consts.tile([P, P], BF16, name="ones")
+        nc.vector.memset(ones[:], 1.0)
+        bias_all = consts.tile([P, 4, WIDTH], F32, name="bias_all")
+        for j in range(4):
+            spread = psum_acc.tile([P, WIDTH], F32, name="acc")
+            nc.tensor.matmul(
+                out=spread[:], lhsT=ones[:], rhs=bias_rows[:, j, :], start=True, stop=True
+            )
+            nc.scalar.copy(out=bias_all[:, j, :], in_=spread[:])
+
+        w_words = consts.tile([P, 10, WIDTH], U32, name="w_words", align_bytes=64)
+        w_scales = consts.tile([P, 10, WIDTH], U8, name="w_scales", align_bytes=64)
+        for j, (w_x, w_h) in enumerate(((W_wf, W_uf), (W_wi, W_ui), (W_wo, W_uo))):
+            for g in range(X_PASSES):
+                piece = W_X + X_PASSES * j + g
+                quantise_weight_piece(
+                    nc,
+                    stage,
+                    w_x[g * K_PASS : (g + 1) * K_PASS, :],
+                    w_words[:, piece, :],
+                    w_scales[:, piece, :],
+                )
+            quantise_weight_piece(nc, stage, w_h, w_words[:, j, :], w_scales[:, j, :])
+        quantise_weight_piece(nc, stage, W_g, w_words[:, W_PROP, :], w_scales[:, W_PROP, :])
+
+        gate_add = consts.tile([P, HALVES, 3, WIDTH], F32, name="gate_add")
+        for half in range(HALVES):
+            for j in range(3):
+                acc = psum_acc.tile([P, WIDTH], F32, name="acc")
+                for g in range(X_PASSES):
+                    piece = W_X + X_PASSES * j + g
+                    nc.tensor.matmul_mx(
+                        out=acc[:],
+                        lhsT=x_words[:, half, g, :].bitcast(FP8X4),
+                        lhsT_scale=x_scales[:, half, g, :],
+                        rhs=w_words[:, piece, :].bitcast(FP8X4),
+                        rhs_scale=w_scales[:, piece, :],
+                        start=(g == 0),
+                        stop=(g == X_PASSES - 1),
+                    )
+                nc.vector.tensor_add(
+                    out=gate_add[:, half, j, :], in0=acc[:], in1=bias_all[:, j, :]
+                )
+
+        for half in range(HALVES):
+            rows = slice(half * P, (half + 1) * P)
+            for s0 in range(0, SLOTS, CHUNK):
+                slots = slice(s0, s0 + CHUNK)
+                h_nat = work.tile([P, CHUNK, WIDTH], BF16, name="h_nat")
+                nc.sync.dma_start(out=h_nat[:], in_=h_state[rows, slots, :])
+                p_nat = work.tile([P, CHUNK, WIDTH], BF16, name="p_nat")
+                nc.sync.dma_start(out=p_nat[:], in_=mem_att[rows, slots, :])
+                m_nat = work.tile([P, CHUNK, WIDTH], BF16, name="m_nat")
+                nc.sync.dma_start(out=m_nat[:], in_=m_state[rows, slots, :])
+
+                grouped = work.tile([P, 2, CHUNK, P, PACK], BF16, name="hp_grouped", align_bytes=64)
+                grouped_pairs = grouped[:].bitcast(F32)
+                for c in range(CHUNK):
+                    turned = psum_t.tile([P, 2, 2, P], F32, name="turned")
+                    for x, nat in enumerate((h_nat, p_nat)):
+                        pairs = nat[:].bitcast(F32)
+                        for u in range(2):
+                            nc.tensor.transpose(
+                                turned[:, x, u, :], pairs[:, c, u * P : (u + 1) * P], ident[:]
+                            )
+                    nc.scalar.copy(
+                        out=grouped_pairs[:, :, c, :, :],
+                        in_=turned[:].rearrange("q x u b -> q x b u"),
+                    )
+                words = work.tile([P, 2, CHUNK, P], U32, name="hp_words", align_bytes=64)
+                scales = work.tile([P, 2, CHUNK, P], U8, name="hp_scales", align_bytes=64)
+                nc.vector.quantize_mx(
+                    out=words[:].rearrange("q x c b -> q (x c b)").bitcast(FP8X4),
+                    scales=scales[:].rearrange("q x c b -> q (x c b)"),
+                    in_=grouped[:].rearrange("q x c b t -> q (x c b t)"),
+                )
+
+                tanh_m = work.tile([P, CHUNK, WIDTH], F32, name="tanh_m")
+                nc.scalar.activation(out=tanh_m[:], in_=m_nat[:], func=FUNC.Tanh)
+                prop = work.tile([P, CHUNK, WIDTH], F32, name="prop")
+                nc.gpsimd.tensor_tensor(
+                    out=prop[:],
+                    in0=p_nat[:],
+                    in1=bias_all[:, 3, :].unsqueeze(1).to_broadcast([P, CHUNK, WIDTH]),
+                    op=ALU.add,
+                )
+
+                forget = work.tile([P, CHUNK, WIDTH], F32, name="forget")
+                in_out = work.tile([P, 2, CHUNK, WIDTH], F32, name="in_out")
+                for c in range(CHUNK):
+                    for piece, x in ((W_F, 0), (W_I, 0), (W_O, 0), (W_PROP, 1)):
+                        acc = psum_acc.tile([P, WIDTH], F32, name="acc")
+                        nc.tensor.matmul_mx(
+                            out=acc[:],
+                            lhsT=words[:, x, c, :].bitcast(FP8X4),
+                            lhsT_scale=scales[:, x, c, :],
+                            rhs=w_words[:, piece, :].bitcast(FP8X4),
+                            rhs_scale=w_scales[:, piece, :],
+                            start=True,
+                            stop=True,
+                        )
+                        if piece == W_F:
+                            nc.vector.tensor_add(
+                                out=forget[:, c, :], in0=acc[:], in1=gate_add[:, half, W_F, :]
+                            )
+                        elif piece == W_PROP:
+                            nc.vector.tensor_add(
+                                out=prop[:, c, :], in0=acc[:], in1=prop[:, c, :]
+                            )
+                        else:
+                            nc.vector.tensor_add(
+                                out=in_out[:, piece - W_I, c, :],
+                                in0=acc[:],
+                                in1=gate_add[:, half, piece, :],
+                            )
+
+                nc.scalar.activation(out=forget[:], in_=forget[:], func=FUNC.Sigmoid)
+                nc.scalar.activation(out=in_out[:], in_=in_out[:], func=FUNC.Sigmoid)
+                nc.vector.tensor_mul(out=forget[:], in0=m_nat[:], in1=forget[:])
+                nc.scalar.activation(out=in_out[:], in_=in_out[:], func=FUNC.Sigmoid)
+                nc.scalar.activation(
+                    out=forget[:], in_=forget[:], func=FUNC.Sigmoid, bias=one_col[:]
+                )
+                nc.vector.tensor_mul(out=prop[:], in0=prop[:], in1=in_out[:, 0, :, :])
+                nc.gpsimd.tensor_tensor(out=forget[:], in0=forget[:], in1=prop[:], op=ALU.add)
+                nc.sync.dma_start(out=out_0[rows, slots, :], in_=forget[:])
+                nc.gpsimd.tensor_tensor(
+                    out=tanh_m[:], in0=tanh_m[:], in1=in_out[:, 1, :, :], op=ALU.mult
+                )
+                nc.sync.dma_start(out=out_1[rows, slots, :], in_=tanh_m[:])

@@ -20,30 +20,45 @@ PACK = 4
 K_PASS = P * PACK
 HALVES = BATCH // P
 X_PASSES = D_IN // K_PASS
-CHUNK = 2
+GROUP = 4
+ROWS = GROUP * P
+BLOCKS = WIDTH // P
+assert BLOCKS == GROUP
+GROUPS_PER_HALF = SLOTS // GROUP
+GROUPS = HALVES * GROUPS_PER_HALF
+STEPS = GROUPS * GROUP
+STEPS_PER_HALF = STEPS // HALVES
 
 FLOPS = 2 * (4 * BATCH * SLOTS * WIDTH * WIDTH + 3 * BATCH * D_IN * WIDTH)
 
-W_F, W_I, W_O, W_PROP = 0, 1, 2, 3
-W_X = 4
+W_UI, W_XI, W_UO, W_XO, W_G, W_XF, W_UF = 0, 1, 3, 4, 6, 7, 9
+N_PIECES = 10
+N_ACROSS = 7
+B_I, B_O, B_G = 0, 1, 2
+
+LOAD_LEAD = 8
+TURN_LEAD = 5
+TANH_LEAD = 12
+ALONG_LAG = 2
+BACK_LAG = 5
+W_LOAD_LEAD, W_REGROUP_LEAD, W_QUANTISE_LEAD = 11, 8, 7
+X_LOAD_LEAD, X_TURN_LEAD, X_QUANTISE_LEAD = 6, 3, 1
+M_LOAD_LEAD = TANH_LEAD + GROUP
+BIAS_STEP = -3
+FIRST_STEP = -M_LOAD_LEAD
+
+LOADED_BUFS = 4
+W_BUFS = 4
+M_BUFS = 6
+ACROSS_BUFS = 2 * BLOCKS
+PROP_BUFS = 3
+ALONG_BUFS = 5
+TANH_BUFS = TANH_LEAD + BACK_LAG + 1
 
 
-def quantise_weight_piece(nc, stage, w_rows, words, scales):
-    raw = stage.tile([P, PACK, WIDTH], BF16, name="raw")
-    nc.sync.dma_start(
-        out=raw[:].rearrange("q (u e) n -> q u e n", u=2),
-        in_=w_rows.rearrange("(u q e) n -> q u e n", u=2, e=2),
-    )
-    grouped = stage.tile([P, WIDTH, PACK], BF16, name="grouped", align_bytes=64)
-    nc.vector.tensor_copy(
-        out=grouped[:].rearrange("q (c i) t -> q c t i", i=4),
-        in_=raw[:].rearrange("q t (c i) -> q c t i", i=4),
-    )
-    nc.vector.quantize_mx(
-        out=words.bitcast(FP8X4),
-        scales=scales,
-        in_=grouped[:].rearrange("q n t -> q (n t)"),
-    )
+def due(step, lead, every, count):
+    number, rest = divmod(step + lead, every)
+    return number if rest == 0 and 0 <= number < count else None
 
 
 def tile_relationalmemorycorecell_pa_t_kernel(
@@ -67,170 +82,403 @@ def tile_relationalmemorycorecell_pa_t_kernel(
     out_1,
 ):
     nc = tc.nc
+    weight_pieces = (
+        W_ui,
+        W_wi[0:K_PASS, :],
+        W_wi[K_PASS:D_IN, :],
+        W_uo,
+        W_wo[0:K_PASS, :],
+        W_wo[K_PASS:D_IN, :],
+        W_g,
+        W_wf[0:K_PASS, :],
+        W_wf[K_PASS:D_IN, :],
+        W_uf,
+    )
     with ExitStack() as pools:
+        pools.enter_context(tc.manual_schedule())
         consts = pools.enter_context(tc.tile_pool(name="consts", bufs=1))
-        stage = pools.enter_context(tc.tile_pool(name="stage", bufs=3))
-        work = pools.enter_context(tc.tile_pool(name="work", bufs=3))
-        psum_t = pools.enter_context(tc.psum_pool(name="psum_t", bufs=2))
-        psum_acc = pools.enter_context(tc.psum_pool(name="psum_acc", bufs=6))
+        work = pools.enter_context(tc.tile_pool(name="work", bufs=2))
+        psum = pools.enter_context(tc.psum_pool(name="psum", bufs=1))
 
-        ident = consts.tile([P, P], F32, name="ident")
-        make_identity(nc, ident[:])
-        one_col = consts.tile([P, 1], F32, name="one_col")
-        nc.vector.memset(one_col[:], 1.0)
+        live = {}
 
-        x_words = consts.tile([P, HALVES, X_PASSES, P], U32, name="x_words", align_bytes=64)
-        x_scales = consts.tile([P, HALVES, X_PASSES, P], U8, name="x_scales", align_bytes=64)
-        for half in range(HALVES):
-            x_nat = stage.tile([P, D_IN], BF16, name="x_nat")
-            nc.sync.dma_start(out=x_nat[:], in_=inputs[half * P : (half + 1) * P, :])
-            x_pairs = x_nat[:].bitcast(F32)
-            x_t = psum_t.tile([P, X_PASSES, 2, P], F32, name="turned")
-            for g in range(X_PASSES):
-                for u in range(2):
-                    first = (2 * g + u) * P
-                    nc.tensor.transpose(x_t[:, g, u, :], x_pairs[:, first : first + P], ident[:])
-            x_grouped = stage.tile([P, X_PASSES, P, PACK], BF16, name="x_grouped", align_bytes=64)
-            nc.vector.tensor_copy(
-                out=x_grouped[:].bitcast(F32), in_=x_t[:].rearrange("q g u b -> q g b u")
+        w_words = consts.tile([P, N_PIECES, WIDTH], U32, name="w_words", align_bytes=64)
+        w_scales = consts.tile([P, N_PIECES, WIDTH], U8, name="w_scales", align_bytes=64)
+        x_words = consts.tile([P, HALVES, X_PASSES, ROWS], U32, name="x_words", align_bytes=64)
+        x_scales = consts.tile([P, HALVES, X_PASSES, ROWS], U8, name="x_scales", align_bytes=64)
+        gate_add = consts.tile([P, HALVES, WIDTH], F32, name="gate_add")
+
+        def where(g):
+            half, quarter = divmod(g, GROUPS_PER_HALF)
+            return slice(half * P, (half + 1) * P), quarter * GROUP
+
+        def mx(acc, stationary, moving, start, stop):
+            nc.tensor.matmul_mx(
+                out=acc,
+                lhsT=stationary[0].bitcast(FP8X4),
+                lhsT_scale=stationary[1],
+                rhs=moving[0].bitcast(FP8X4),
+                rhs_scale=moving[1],
+                start=start,
+                stop=stop,
             )
+
+        def weight(piece, first=0, columns=WIDTH):
+            cols = slice(first, first + columns)
+            return w_words[:, piece, cols], w_scales[:, piece, cols]
+
+        def load_m(g):
+            batch, first = where(g)
+            m_rows = work.tile([P, GROUP, WIDTH], BF16, name="m_rows", bufs=M_BUFS)
+            nc.scalar.dma_start(out=m_rows[:], in_=m_state[batch, first : first + GROUP, :])
+            live["m", g] = m_rows
+
+        def load_group(g):
+            batch, first = where(g)
+            for kind, source in (("h", h_state), ("p", mem_att)):
+                loaded = work.tile([P, GROUP, WIDTH], BF16, name="loaded", bufs=LOADED_BUFS)
+                nc.sync.dma_start(out=loaded[:], in_=source[batch, first : first + GROUP, :])
+                live[kind, g] = loaded
+
+        def load_weight(piece):
+            w_rows = work.tile([P, PACK, WIDTH], BF16, name="w_rows", bufs=W_BUFS)
+            nc.sync.dma_start(
+                out=w_rows[:].rearrange("q (u e) n -> q u e n", u=2),
+                in_=weight_pieces[piece].rearrange("(u q e) n -> q u e n", u=2, e=2),
+            )
+            live["w", piece] = w_rows
+
+        def load_x(half):
+            x_rows = work.tile([P, D_IN], BF16, name="x_rows", bufs=1)
+            nc.sync.dma_start(out=x_rows[:], in_=inputs[half * P : (half + 1) * P, :])
+            live["x", half] = x_rows
+
+        def regroup_weight(piece):
+            grouped = work.tile([P, WIDTH, PACK], BF16, name="w_grouped", align_bytes=64)
+            if piece < N_ACROSS:
+                nc.vector.tensor_copy(
+                    out=grouped[:].rearrange("q (u e j) t -> q u e j t", u=2, e=2),
+                    in_=live["w", piece][:].rearrange("q t (u j e) -> q u e j t", u=2, e=2),
+                )
+            else:
+                nc.vector.tensor_copy(
+                    out=grouped[:].rearrange("q (c i) t -> q c t i", i=4),
+                    in_=live["w", piece][:].rearrange("q t (c i) -> q c t i", i=4),
+                )
+            live["w_grouped", piece] = grouped
+
+        def quantise_weight(piece):
             nc.vector.quantize_mx(
-                out=x_words[:, half, :, :].rearrange("q g b -> q (g b)").bitcast(FP8X4),
-                scales=x_scales[:, half, :, :].rearrange("q g b -> q (g b)"),
-                in_=x_grouped[:].rearrange("q g b t -> q (g b t)"),
+                out=w_words[:, piece, :].bitcast(FP8X4),
+                scales=w_scales[:, piece, :],
+                in_=live["w_grouped", piece][:].rearrange("q n t -> q (n t)"),
+            )
+
+        def out_of_psum(step):
+            return nc.scalar.copy if step < 0 else nc.vector.tensor_copy
+
+        def turn_x(half, step):
+            pairs = live["x", half][:].bitcast(F32)
+            turned = psum.tile([P, X_PASSES, 2, P], F32, name="turned", bufs=2)
+            for a in range(X_PASSES):
+                for u in range(2):
+                    first = (2 * a + u) * P
+                    nc.tensor.transpose(turned[:, a, u, :], pairs[:, first : first + P], ident[:])
+            grouped = work.tile(
+                [P, X_PASSES, P, PACK], BF16, name="x_grouped", align_bytes=64, bufs=1
+            )
+            out_of_psum(step)(
+                out=grouped[:].bitcast(F32), in_=turned[:].rearrange("q a u b -> q a b u")
+            )
+            live["x_grouped", half] = grouped
+
+        def quantise_x(half):
+            for a in range(X_PASSES):
+                for c in range(GROUP):
+                    cols = slice(c * P, (c + 1) * P)
+                    nc.vector.quantize_mx(
+                        out=x_words[:, half, a, cols].bitcast(FP8X4),
+                        scales=x_scales[:, half, a, cols],
+                        in_=live["x_grouped", half][:, a, :, :].rearrange("q b t -> q (b t)"),
+                    )
+
+        def x_operand(half, a, columns=ROWS):
+            return x_words[:, half, a, 0:columns], x_scales[:, half, a, 0:columns]
+
+        def gate_terms(half):
+            acc = psum.tile([P, WIDTH], F32, name="acc_f")
+            for a in range(X_PASSES):
+                mx(acc[:], x_operand(half, a, P), weight(W_XF + a), a == 0, a == X_PASSES - 1)
+            nc.vector.tensor_add(out=gate_add[:, half, :], in0=acc[:], in1=bias_f[:])
+
+        def turn(w):
+            g, quarter = divmod(w, 4)
+            kind = "h" if quarter < 2 else "p"
+            first = 2 * (quarter % 2)
+            pairs = live[kind, g][:].bitcast(F32)
+            turned = psum.tile([P, 2, 2, P], F32, name="turned", bufs=2)
+            for c in range(2):
+                for u in range(2):
+                    nc.tensor.transpose(
+                        turned[:, c, u, :], pairs[:, first + c, u * P : (u + 1) * P], ident[:]
+                    )
+            live["turned", w] = turned
+
+        def regroup(w, step):
+            g, quarter = divmod(w, 4)
+            kind = "h" if quarter < 2 else "p"
+            first = 2 * (quarter % 2)
+            if first == 0:
+                live[kind + "_grouped", g] = work.tile(
+                    [P, GROUP, P, PACK], BF16, name=kind + "_grouped", align_bytes=64
+                )
+            out_of_psum(step)(
+                out=live[kind + "_grouped", g][:].bitcast(F32)[:, first : first + 2, :, :],
+                in_=live["turned", w][:].rearrange("q c u b -> q c b u"),
+            )
+
+        def quantise(kind, g):
+            words = work.tile([P, ROWS], U32, name=kind + "_words", align_bytes=64)
+            scales = work.tile([P, ROWS], U8, name=kind + "_scales", align_bytes=64)
+            nc.vector.quantize_mx(
+                out=words[:].bitcast(FP8X4),
+                scales=scales[:],
+                in_=live[kind + "_grouped", g][:].rearrange("q c b t -> q (c b t)"),
+            )
+            live[kind + "_mx", g] = (words, scales)
+
+        def rows_operand(kind, g, first=0, columns=ROWS):
+            words, scales = live[kind + "_mx", g]
+            return words[:, first : first + columns], scales[:, first : first + columns]
+
+        def gate_across(i, kind, u_piece, x_piece):
+            g, t = divmod(i, BLOCKS)
+            acc = psum.tile([P, ROWS], F32, name="acc_" + kind)
+            mx(acc[:], weight(u_piece, t * P, P), rows_operand("h", g), True, False)
+            for a in range(X_PASSES):
+                mx(
+                    acc[:],
+                    weight(x_piece + a, t * P, P),
+                    x_operand(g // GROUPS_PER_HALF, a),
+                    False,
+                    a == X_PASSES - 1,
+                )
+            live["acc_" + kind, i] = acc
+
+        def prop_across(i):
+            g, t = divmod(i, BLOCKS)
+            acc = psum.tile([P, ROWS], F32, name="acc_p")
+            mx(acc[:], weight(W_G, t * P, P), rows_operand("p", g), True, True)
+            live["acc_p", i] = acc
+
+        def bias_of(place, t):
+            return bias_col[:, place * BLOCKS + t : place * BLOCKS + t + 1]
+
+        def first_sigmoid(i, kind, place):
+            gate = work.tile([P, ROWS], F32, name="gate_" + kind, bufs=ACROSS_BUFS)
+            nc.scalar.activation(
+                out=gate[:],
+                in_=live["acc_" + kind, i][:],
+                func=FUNC.Sigmoid,
+                bias=bias_of(place, i % BLOCKS),
+            )
+            live[kind, i] = gate
+
+        def second_sigmoid(i, kind):
+            nc.scalar.activation(out=live[kind, i][:], in_=live[kind, i][:], func=FUNC.Sigmoid)
+
+        def prop_sum(i):
+            g, t = divmod(i, BLOCKS)
+            prop = work.tile([P, ROWS], F32, name="prop", bufs=PROP_BUFS)
+            nc.vector.scalar_tensor_tensor(
+                out=prop[:],
+                in0=live["acc_p", i][:],
+                scalar=bias_of(B_G, t),
+                in1=live["p_grouped", g][:, :, :, t].rearrange("q c b -> q (c b)"),
+                op0=ALU.add,
+                op1=ALU.add,
+            )
+            live["prop", i] = prop
+
+        def prop_times_gate(i):
+            nc.gpsimd.tensor_tensor(
+                out=live["i", i][:], in0=live["prop", i][:], in1=live["i", i][:], op=ALU.mult
+            )
+
+        def back(i, kind):
+            g, c = divmod(i, GROUP)
+            bank = psum.tile([P, BLOCKS, P], F32, name="back_" + kind)
+            for t in range(BLOCKS):
+                nc.tensor.transpose(
+                    bank[:, t, :], live[kind, g * BLOCKS + t][:, c * P : (c + 1) * P], ident[:]
+                )
+            live["back_" + kind, i] = bank[:].rearrange("b (u e) j -> b u j e", u=2)
+
+        def as_blocks(tile):
+            return tile[:].rearrange("b (u j e) -> b u j e", u=2, e=2)
+
+        def tanh_of_m(i):
+            g, c = divmod(i, GROUP)
+            tanh_m = work.tile([P, WIDTH], F32, name="tanh_m", bufs=TANH_BUFS)
+            nc.scalar.activation(out=tanh_m[:], in_=live["m", g][:, c, :], func=FUNC.Tanh)
+            live["tanh", i] = tanh_m
+
+        def forget_product(i):
+            g, c = divmod(i, GROUP)
+            acc = psum.tile([P, WIDTH], F32, name="acc_f")
+            mx(acc[:], rows_operand("h", g, c * P, P), weight(W_UF), True, True)
+            live["acc_f", i] = acc
+
+        def forget_sum(i):
+            forget = work.tile([P, WIDTH], F32, name="forget", bufs=ALONG_BUFS)
+            nc.vector.tensor_add(
+                out=forget[:], in0=live["acc_f", i][:], in1=gate_add[:, i // STEPS_PER_HALF, :]
+            )
+            live["f", i] = forget
+
+        def forget_sigmoid(i):
+            nc.scalar.activation(out=live["f", i][:], in_=live["f", i][:], func=FUNC.Sigmoid)
+
+        def forget_times_m(i):
+            g, c = divmod(i, GROUP)
+            nc.gpsimd.tensor_tensor(
+                out=live["f", i][:], in0=live["m", g][:, c, :], in1=live["f", i][:], op=ALU.mult
+            )
+
+        def kept_sigmoid(i):
+            nc.scalar.activation(
+                out=live["f", i][:], in_=live["f", i][:], func=FUNC.Sigmoid, bias=one_col[:]
+            )
+
+        def finish(i):
+            g, c = divmod(i, GROUP)
+            batch, first = where(g)
+            slot = first + c
+            nc.vector.tensor_tensor(
+                out=as_blocks(live["tanh", i]),
+                in0=live["back_o", i],
+                in1=as_blocks(live["tanh", i]),
+                op=ALU.mult,
+            )
+            nc.sync.dma_start(out=out_1[batch, slot, :], in_=live["tanh", i][:])
+            nc.vector.tensor_tensor(
+                out=as_blocks(live["f", i]),
+                in0=live["back_i", i],
+                in1=as_blocks(live["f", i]),
+                op=ALU.add,
+            )
+            nc.sync.dma_start(out=out_0[batch, slot, :], in_=live["f", i][:])
+
+        def spread_biases():
+            spread = psum.tile([P, WIDTH], F32, name="acc_f")
+            nc.tensor.matmul(
+                out=spread[:], lhsT=ones[:], rhs=bias_rows[:, 3, :], start=True, stop=True
+            )
+            nc.scalar.copy(out=bias_f[:], in_=spread[:])
+            bias_pairs = bias_rows[:].bitcast(F32)
+            for place, name in ((B_I, "back_i"), (B_O, "back_o"), (B_G, "acc_p")):
+                bank = psum.tile([P, BLOCKS, P], F32, name=name)
+                for u in range(2):
+                    nc.tensor.transpose(
+                        bank[:, u, :], bias_pairs[:, place, u * P : (u + 1) * P], ident[:]
+                    )
+                nc.scalar.copy(out=bias_words[:, place, :], in_=bank[:, 0:2, 0])
+            nc.vector.tensor_copy(
+                out=bias_col[:], in_=bias_words[:].rearrange("q g u -> q (g u)").bitcast(BF16)
             )
 
         bias_rows = consts.tile([P, 4, WIDTH], BF16, name="bias_rows")
         nc.vector.memset(bias_rows[:], 0.0)
-        for j, bias in enumerate((b_uf, b_ui, b_uo, b_g)):
+        for j, bias in enumerate((b_ui, b_uo, b_g, b_uf)):
             nc.scalar.dma_start(out=bias_rows[0:1, j, :], in_=bias.unsqueeze(0))
+        bias_f = consts.tile([P, WIDTH], F32, name="bias_f")
+        bias_words = consts.tile([P, 3, 2], F32, name="bias_words")
+        bias_col = consts.tile([P, 3 * BLOCKS], F32, name="bias_col")
+        ident = consts.tile([P, P], F32, name="ident")
+        make_identity(nc, ident[:])
+        one_col = consts.tile([P, 1], F32, name="one_col")
+        nc.vector.memset(one_col[:], 1.0)
         ones = consts.tile([P, P], BF16, name="ones")
         nc.vector.memset(ones[:], 1.0)
-        bias_all = consts.tile([P, 4, WIDTH], F32, name="bias_all")
-        for j in range(4):
-            spread = psum_acc.tile([P, WIDTH], F32, name="acc")
-            nc.tensor.matmul(
-                out=spread[:], lhsT=ones[:], rhs=bias_rows[:, j, :], start=True, stop=True
-            )
-            nc.scalar.copy(out=bias_all[:, j, :], in_=spread[:])
 
-        w_words = consts.tile([P, 10, WIDTH], U32, name="w_words", align_bytes=64)
-        w_scales = consts.tile([P, 10, WIDTH], U8, name="w_scales", align_bytes=64)
-        for j, (w_x, w_h) in enumerate(((W_wf, W_uf), (W_wi, W_ui), (W_wo, W_uo))):
-            for g in range(X_PASSES):
-                piece = W_X + X_PASSES * j + g
-                quantise_weight_piece(
-                    nc,
-                    stage,
-                    w_x[g * K_PASS : (g + 1) * K_PASS, :],
-                    w_words[:, piece, :],
-                    w_scales[:, piece, :],
-                )
-            quantise_weight_piece(nc, stage, w_h, w_words[:, j, :], w_scales[:, j, :])
-        quantise_weight_piece(nc, stage, W_g, w_words[:, W_PROP, :], w_scales[:, W_PROP, :])
+        for n in range(FIRST_STEP, STEPS + BACK_LAG + 1):
+            multiplied = n if 0 <= n < STEPS else None
+            along = due(n, -ALONG_LAG, 1, STEPS)
+            finished = due(n, -BACK_LAG, 1, STEPS)
+            turning = due(n, TURN_LEAD, 1, STEPS)
 
-        gate_add = consts.tile([P, HALVES, 3, WIDTH], F32, name="gate_add")
-        for half in range(HALVES):
-            for j in range(3):
-                acc = psum_acc.tile([P, WIDTH], F32, name="acc")
-                for g in range(X_PASSES):
-                    piece = W_X + X_PASSES * j + g
-                    nc.tensor.matmul_mx(
-                        out=acc[:],
-                        lhsT=x_words[:, half, g, :].bitcast(FP8X4),
-                        lhsT_scale=x_scales[:, half, g, :],
-                        rhs=w_words[:, piece, :].bitcast(FP8X4),
-                        rhs_scale=w_scales[:, piece, :],
-                        start=(g == 0),
-                        stop=(g == X_PASSES - 1),
-                    )
-                nc.vector.tensor_add(
-                    out=gate_add[:, half, j, :], in0=acc[:], in1=bias_all[:, j, :]
-                )
+            piece = due(n, W_LOAD_LEAD, 1, N_PIECES)
+            if piece is not None:
+                load_weight(piece)
+            half = due(n, X_LOAD_LEAD, STEPS_PER_HALF, HALVES)
+            if half is not None:
+                load_x(half)
+            g = due(n, LOAD_LEAD, GROUP, GROUPS)
+            if g is not None:
+                load_group(g)
+            g = due(n, M_LOAD_LEAD, GROUP, GROUPS)
+            if g is not None:
+                load_m(g)
 
-        for half in range(HALVES):
-            rows = slice(half * P, (half + 1) * P)
-            for s0 in range(0, SLOTS, CHUNK):
-                slots = slice(s0, s0 + CHUNK)
-                h_nat = work.tile([P, CHUNK, WIDTH], BF16, name="h_nat")
-                nc.sync.dma_start(out=h_nat[:], in_=h_state[rows, slots, :])
-                p_nat = work.tile([P, CHUNK, WIDTH], BF16, name="p_nat")
-                nc.sync.dma_start(out=p_nat[:], in_=mem_att[rows, slots, :])
-                m_nat = work.tile([P, CHUNK, WIDTH], BF16, name="m_nat")
-                nc.sync.dma_start(out=m_nat[:], in_=m_state[rows, slots, :])
+            piece = due(n, W_REGROUP_LEAD, 1, N_PIECES)
+            if piece is not None:
+                regroup_weight(piece)
+            piece = due(n, W_QUANTISE_LEAD, 1, N_PIECES)
+            if piece is not None:
+                quantise_weight(piece)
 
-                grouped = work.tile([P, 2, CHUNK, P, PACK], BF16, name="hp_grouped", align_bytes=64)
-                grouped_pairs = grouped[:].bitcast(F32)
-                for c in range(CHUNK):
-                    turned = psum_t.tile([P, 2, 2, P], F32, name="turned")
-                    for x, nat in enumerate((h_nat, p_nat)):
-                        pairs = nat[:].bitcast(F32)
-                        for u in range(2):
-                            nc.tensor.transpose(
-                                turned[:, x, u, :], pairs[:, c, u * P : (u + 1) * P], ident[:]
-                            )
-                    nc.scalar.copy(
-                        out=grouped_pairs[:, :, c, :, :],
-                        in_=turned[:].rearrange("q x u b -> q x b u"),
-                    )
-                words = work.tile([P, 2, CHUNK, P], U32, name="hp_words", align_bytes=64)
-                scales = work.tile([P, 2, CHUNK, P], U8, name="hp_scales", align_bytes=64)
-                nc.vector.quantize_mx(
-                    out=words[:].rearrange("q x c b -> q (x c b)").bitcast(FP8X4),
-                    scales=scales[:].rearrange("q x c b -> q (x c b)"),
-                    in_=grouped[:].rearrange("q x c b t -> q (x c b t)"),
-                )
+            if finished is not None:
+                back(finished, "o")
+                back(finished, "i")
+            if turning is not None:
+                turn(turning)
+            half = due(n, X_TURN_LEAD, STEPS_PER_HALF, HALVES)
+            if half is not None:
+                turn_x(half, n)
+            if n == BIAS_STEP:
+                spread_biases()
+            if finished is not None:
+                finish(finished)
+            if turning is not None:
+                regroup(turning, n)
+            half = due(n, X_QUANTISE_LEAD, STEPS_PER_HALF, HALVES)
+            if half is not None:
+                quantise_x(half)
 
-                tanh_m = work.tile([P, CHUNK, WIDTH], F32, name="tanh_m")
-                nc.scalar.activation(out=tanh_m[:], in_=m_nat[:], func=FUNC.Tanh)
-                prop = work.tile([P, CHUNK, WIDTH], F32, name="prop")
-                nc.gpsimd.tensor_tensor(
-                    out=prop[:],
-                    in0=p_nat[:],
-                    in1=bias_all[:, 3, :].unsqueeze(1).to_broadcast([P, CHUNK, WIDTH]),
-                    op=ALU.add,
-                )
+            if multiplied is not None:
+                gate_across(n, "i", W_UI, W_XI)
+                gate_across(n, "o", W_UO, W_XO)
+                prop_across(n)
+            half = due(n, -(ALONG_LAG - 1), STEPS_PER_HALF, HALVES)
+            if half is not None:
+                gate_terms(half)
+            if along is not None:
+                forget_product(along)
 
-                forget = work.tile([P, CHUNK, WIDTH], F32, name="forget")
-                in_out = work.tile([P, 2, CHUNK, WIDTH], F32, name="in_out")
-                for c in range(CHUNK):
-                    for piece, x in ((W_F, 0), (W_I, 0), (W_O, 0), (W_PROP, 1)):
-                        acc = psum_acc.tile([P, WIDTH], F32, name="acc")
-                        nc.tensor.matmul_mx(
-                            out=acc[:],
-                            lhsT=words[:, x, c, :].bitcast(FP8X4),
-                            lhsT_scale=scales[:, x, c, :],
-                            rhs=w_words[:, piece, :].bitcast(FP8X4),
-                            rhs_scale=w_scales[:, piece, :],
-                            start=True,
-                            stop=True,
-                        )
-                        if piece == W_F:
-                            nc.vector.tensor_add(
-                                out=forget[:, c, :], in0=acc[:], in1=gate_add[:, half, W_F, :]
-                            )
-                        elif piece == W_PROP:
-                            nc.vector.tensor_add(
-                                out=prop[:, c, :], in0=acc[:], in1=prop[:, c, :]
-                            )
-                        else:
-                            nc.vector.tensor_add(
-                                out=in_out[:, piece - W_I, c, :],
-                                in0=acc[:],
-                                in1=gate_add[:, half, piece, :],
-                            )
+            if multiplied is not None:
+                first_sigmoid(n, "i", B_I)
+                first_sigmoid(n, "o", B_O)
+                prop_sum(n)
+            if along is not None:
+                forget_sum(along)
+            g = due(n, TURN_LEAD - 2, GROUP, GROUPS)
+            if g is not None:
+                quantise("h", g)
+            g = due(n, TURN_LEAD - 4, GROUP, GROUPS)
+            if g is not None:
+                quantise("p", g)
 
-                nc.scalar.activation(out=forget[:], in_=forget[:], func=FUNC.Sigmoid)
-                nc.scalar.activation(out=in_out[:], in_=in_out[:], func=FUNC.Sigmoid)
-                nc.vector.tensor_mul(out=forget[:], in0=m_nat[:], in1=forget[:])
-                nc.scalar.activation(out=in_out[:], in_=in_out[:], func=FUNC.Sigmoid)
-                nc.scalar.activation(
-                    out=forget[:], in_=forget[:], func=FUNC.Sigmoid, bias=one_col[:]
-                )
-                nc.vector.tensor_mul(out=prop[:], in0=prop[:], in1=in_out[:, 0, :, :])
-                nc.gpsimd.tensor_tensor(out=forget[:], in0=forget[:], in1=prop[:], op=ALU.add)
-                nc.sync.dma_start(out=out_0[rows, slots, :], in_=forget[:])
-                nc.gpsimd.tensor_tensor(
-                    out=tanh_m[:], in0=tanh_m[:], in1=in_out[:, 1, :, :], op=ALU.mult
-                )
-                nc.sync.dma_start(out=out_1[rows, slots, :], in_=tanh_m[:])
+            if due(n, -(ALONG_LAG + 1), 1, STEPS) is not None:
+                forget_sigmoid(n - ALONG_LAG - 1)
+            if multiplied is not None:
+                second_sigmoid(n, "i")
+                second_sigmoid(n, "o")
+            if due(n, -(ALONG_LAG + 2), 1, STEPS) is not None:
+                kept_sigmoid(n - ALONG_LAG - 2)
+            if due(n, TANH_LEAD, 1, STEPS) is not None:
+                tanh_of_m(n + TANH_LEAD)
+
+            if due(n, -1, 1, STEPS) is not None:
+                prop_times_gate(n - 1)
+            if due(n, -(ALONG_LAG + 1), 1, STEPS) is not None:
+                forget_times_m(n - ALONG_LAG - 1)

@@ -29,6 +29,8 @@ GROUPS = HALVES * GROUPS_PER_HALF
 STEPS = GROUPS * GROUP
 STEPS_PER_HALF = STEPS // HALVES
 
+FORGET_BIAS = 1.0
+
 FLOPS = 2 * (4 * BATCH * SLOTS * WIDTH * WIDTH + 3 * BATCH * D_IN * WIDTH)
 
 W_UI, W_XI, W_UO, W_XO, W_G, W_XF, W_UF = 0, 1, 3, 4, 6, 7, 9
@@ -38,18 +40,20 @@ B_I, B_O, B_G = 0, 1, 2
 
 LOAD_LEAD = 8
 TURN_LEAD = 5
-TANH_LEAD = 12
+TANH_LEAD = 20
 ALONG_LAG = 2
 BACK_LAG = 5
 W_LOAD_LEAD, W_REGROUP_LEAD, W_QUANTISE_LEAD = 11, 8, 7
-X_LOAD_LEAD, X_TURN_LEAD, X_QUANTISE_LEAD = 6, 3, 1
-M_LOAD_LEAD = TANH_LEAD + GROUP
-BIAS_STEP = -3
+X_LOAD_LEAD, X_TURN_LEAD, X_QUANTISE_LEAD = 9, 6, 4
+M_LOAD_LEAD = TANH_LEAD + 2 * GROUP
+M_AGAIN_LEAD = GROUP - (ALONG_LAG + 1)
+BIAS_LOAD_STEP, BIAS_STEP = -12, -3
 FIRST_STEP = -M_LOAD_LEAD
 
 LOADED_BUFS = 4
 W_BUFS = 4
-M_BUFS = 6
+GROUPED_BUFS = {"h": 1, "p": 2}
+M_BUFS = 3
 ACROSS_BUFS = 2 * BLOCKS
 PROP_BUFS = 3
 ALONG_BUFS = 5
@@ -133,6 +137,12 @@ def tile_relationalmemorycorecell_pa_t_kernel(
             nc.scalar.dma_start(out=m_rows[:], in_=m_state[batch, first : first + GROUP, :])
             live["m", g] = m_rows
 
+        def load_m_again(g):
+            batch, first = where(g)
+            m_again = work.tile([P, GROUP, WIDTH], BF16, name="m_again")
+            nc.sync.dma_start(out=m_again[:], in_=m_state[batch, first : first + GROUP, :])
+            live["m_again", g] = m_again
+
         def load_group(g):
             batch, first = where(g)
             for kind, source in (("h", h_state), ("p", mem_att)):
@@ -174,10 +184,10 @@ def tile_relationalmemorycorecell_pa_t_kernel(
                 in_=live["w_grouped", piece][:].rearrange("q n t -> q (n t)"),
             )
 
-        def out_of_psum(step):
-            return nc.scalar.copy if step < 0 else nc.vector.tensor_copy
+        def out_of_psum(number):
+            return nc.scalar.copy if number == 0 else nc.vector.tensor_copy
 
-        def turn_x(half, step):
+        def turn_x(half):
             pairs = live["x", half][:].bitcast(F32)
             turned = psum.tile([P, X_PASSES, 2, P], F32, name="turned", bufs=2)
             for a in range(X_PASSES):
@@ -187,7 +197,7 @@ def tile_relationalmemorycorecell_pa_t_kernel(
             grouped = work.tile(
                 [P, X_PASSES, P, PACK], BF16, name="x_grouped", align_bytes=64, bufs=1
             )
-            out_of_psum(step)(
+            out_of_psum(half)(
                 out=grouped[:].bitcast(F32), in_=turned[:].rearrange("q a u b -> q a b u")
             )
             live["x_grouped", half] = grouped
@@ -224,15 +234,19 @@ def tile_relationalmemorycorecell_pa_t_kernel(
                     )
             live["turned", w] = turned
 
-        def regroup(w, step):
+        def regroup(w):
             g, quarter = divmod(w, 4)
             kind = "h" if quarter < 2 else "p"
             first = 2 * (quarter % 2)
             if first == 0:
                 live[kind + "_grouped", g] = work.tile(
-                    [P, GROUP, P, PACK], BF16, name=kind + "_grouped", align_bytes=64
+                    [P, GROUP, P, PACK],
+                    BF16,
+                    name=kind + "_grouped",
+                    align_bytes=64,
+                    bufs=GROUPED_BUFS[kind],
                 )
-            out_of_psum(step)(
+            out_of_psum(g)(
                 out=live[kind + "_grouped", g][:].bitcast(F32)[:, first : first + 2, :, :],
                 in_=live["turned", w][:].rearrange("q c u b -> q c b u"),
             )
@@ -342,12 +356,15 @@ def tile_relationalmemorycorecell_pa_t_kernel(
         def forget_times_m(i):
             g, c = divmod(i, GROUP)
             nc.gpsimd.tensor_tensor(
-                out=live["f", i][:], in0=live["m", g][:, c, :], in1=live["f", i][:], op=ALU.mult
+                out=live["f", i][:],
+                in0=live["m_again", g][:, c, :],
+                in1=live["f", i][:],
+                op=ALU.mult,
             )
 
         def kept_sigmoid(i):
             nc.scalar.activation(
-                out=live["f", i][:], in_=live["f", i][:], func=FUNC.Sigmoid, bias=one_col[:]
+                out=live["f", i][:], in_=live["f", i][:], func=FUNC.Sigmoid, bias=FORGET_BIAS
             )
 
         def finish(i):
@@ -369,6 +386,10 @@ def tile_relationalmemorycorecell_pa_t_kernel(
             )
             nc.sync.dma_start(out=out_0[batch, slot, :], in_=live["f", i][:])
 
+        def load_biases():
+            for j, bias in enumerate((b_ui, b_uo, b_g, b_uf)):
+                nc.scalar.dma_start(out=bias_rows[0:1, j, :], in_=bias.unsqueeze(0))
+
         def spread_biases():
             spread = psum.tile([P, WIDTH], F32, name="acc_f")
             nc.tensor.matmul(
@@ -383,21 +404,17 @@ def tile_relationalmemorycorecell_pa_t_kernel(
                         bank[:, u, :], bias_pairs[:, place, u * P : (u + 1) * P], ident[:]
                     )
                 nc.scalar.copy(out=bias_words[:, place, :], in_=bank[:, 0:2, 0])
-            nc.vector.tensor_copy(
+            nc.scalar.copy(
                 out=bias_col[:], in_=bias_words[:].rearrange("q g u -> q (g u)").bitcast(BF16)
             )
 
         bias_rows = consts.tile([P, 4, WIDTH], BF16, name="bias_rows")
         nc.vector.memset(bias_rows[:], 0.0)
-        for j, bias in enumerate((b_ui, b_uo, b_g, b_uf)):
-            nc.scalar.dma_start(out=bias_rows[0:1, j, :], in_=bias.unsqueeze(0))
         bias_f = consts.tile([P, WIDTH], F32, name="bias_f")
         bias_words = consts.tile([P, 3, 2], F32, name="bias_words")
         bias_col = consts.tile([P, 3 * BLOCKS], F32, name="bias_col")
         ident = consts.tile([P, P], F32, name="ident")
         make_identity(nc, ident[:])
-        one_col = consts.tile([P, 1], F32, name="one_col")
-        nc.vector.memset(one_col[:], 1.0)
         ones = consts.tile([P, P], BF16, name="ones")
         nc.vector.memset(ones[:], 1.0)
 
@@ -419,6 +436,11 @@ def tile_relationalmemorycorecell_pa_t_kernel(
             g = due(n, M_LOAD_LEAD, GROUP, GROUPS)
             if g is not None:
                 load_m(g)
+            if n == BIAS_LOAD_STEP:
+                load_biases()
+            g = due(n, M_AGAIN_LEAD, GROUP, GROUPS)
+            if g is not None:
+                load_m_again(g)
 
             piece = due(n, W_REGROUP_LEAD, 1, N_PIECES)
             if piece is not None:
@@ -434,13 +456,13 @@ def tile_relationalmemorycorecell_pa_t_kernel(
                 turn(turning)
             half = due(n, X_TURN_LEAD, STEPS_PER_HALF, HALVES)
             if half is not None:
-                turn_x(half, n)
+                turn_x(half)
             if n == BIAS_STEP:
                 spread_biases()
             if finished is not None:
                 finish(finished)
             if turning is not None:
-                regroup(turning, n)
+                regroup(turning)
             half = due(n, X_QUANTISE_LEAD, STEPS_PER_HALF, HALVES)
             if half is not None:
                 quantise_x(half)

@@ -35,29 +35,32 @@ FLOPS = 2 * (4 * BATCH * SLOTS * WIDTH * WIDTH + 3 * BATCH * D_IN * WIDTH)
 
 W_UI, W_XI, W_UO, W_XO, W_G, W_XF, W_UF = 0, 1, 3, 4, 6, 7, 9
 N_PIECES = 10
+SCALAR_S_PIECE = 1
 N_ACROSS = 7
 B_I, B_O, B_G = 0, 1, 2
 
 LOAD_LEAD = 8
 TURN_LEAD = 5
-TANH_LEAD = 20
+TANH_LEAD = 8
 ALONG_LAG = 2
 BACK_LAG = 5
 W_LOAD_LEAD, W_REGROUP_LEAD, W_QUANTISE_LEAD = 11, 8, 7
 X_LOAD_LEAD, X_TURN_LEAD, X_QUANTISE_LEAD = 9, 6, 4
-M_LOAD_LEAD = TANH_LEAD + 2 * GROUP
-M_AGAIN_LEAD = GROUP - (ALONG_LAG + 1)
-BIAS_LOAD_STEP, BIAS_STEP = -12, -3
-FIRST_STEP = -M_LOAD_LEAD
+M_LOAD_LEAD = TANH_LEAD + GROUP
+BIAS_STEP = -3
+FIRST_STEP = -max(M_LOAD_LEAD, W_LOAD_LEAD)
 
 LOADED_BUFS = 4
 W_BUFS = 4
-GROUPED_BUFS = {"h": 1, "p": 2}
-M_BUFS = 3
+W_FIRST = 2
+M_BUFS = 5
 ACROSS_BUFS = 2 * BLOCKS
 PROP_BUFS = 3
 ALONG_BUFS = 5
 TANH_BUFS = TANH_LEAD + BACK_LAG + 1
+
+
+GPSIMD_PIECES = (slice(0, WIDTH // 2), slice(WIDTH // 2, WIDTH))
 
 
 def due(step, lead, every, count):
@@ -134,14 +137,8 @@ def tile_relationalmemorycorecell_pa_t_kernel(
         def load_m(g):
             batch, first = where(g)
             m_rows = work.tile([P, GROUP, WIDTH], BF16, name="m_rows", bufs=M_BUFS)
-            nc.scalar.dma_start(out=m_rows[:], in_=m_state[batch, first : first + GROUP, :])
+            nc.sync.dma_start(out=m_rows[:], in_=m_state[batch, first : first + GROUP, :])
             live["m", g] = m_rows
-
-        def load_m_again(g):
-            batch, first = where(g)
-            m_again = work.tile([P, GROUP, WIDTH], BF16, name="m_again")
-            nc.sync.dma_start(out=m_again[:], in_=m_state[batch, first : first + GROUP, :])
-            live["m_again", g] = m_again
 
         def load_group(g):
             batch, first = where(g)
@@ -166,10 +163,13 @@ def tile_relationalmemorycorecell_pa_t_kernel(
         def regroup_weight(piece):
             grouped = work.tile([P, WIDTH, PACK], BF16, name="w_grouped", align_bytes=64)
             if piece < N_ACROSS:
-                nc.vector.tensor_copy(
-                    out=grouped[:].rearrange("q (u e j) t -> q u e j t", u=2, e=2),
-                    in_=live["w", piece][:].rearrange("q t (u j e) -> q u e j t", u=2, e=2),
-                )
+                by_block = grouped[:].rearrange("q (u e j) t -> q u e j t", u=2, e=2)
+                by_column = live["w", piece][:].rearrange("q t (u j e) -> q u e j t", u=2, e=2)
+                if piece % 3 == SCALAR_S_PIECE:
+                    for u in range(2):
+                        nc.scalar.copy(out=by_block[:, u], in_=by_column[:, u])
+                else:
+                    nc.vector.tensor_copy(out=by_block, in_=by_column)
             else:
                 nc.vector.tensor_copy(
                     out=grouped[:].rearrange("q (c i) t -> q c t i", i=4),
@@ -240,11 +240,7 @@ def tile_relationalmemorycorecell_pa_t_kernel(
             first = 2 * (quarter % 2)
             if first == 0:
                 live[kind + "_grouped", g] = work.tile(
-                    [P, GROUP, P, PACK],
-                    BF16,
-                    name=kind + "_grouped",
-                    align_bytes=64,
-                    bufs=GROUPED_BUFS[kind],
+                    [P, GROUP, P, PACK], BF16, name=kind + "_grouped", align_bytes=64
                 )
             out_of_psum(g)(
                 out=live[kind + "_grouped", g][:].bitcast(F32)[:, first : first + 2, :, :],
@@ -315,9 +311,13 @@ def tile_relationalmemorycorecell_pa_t_kernel(
             live["prop", i] = prop
 
         def prop_times_gate(i):
-            nc.gpsimd.tensor_tensor(
-                out=live["i", i][:], in0=live["prop", i][:], in1=live["i", i][:], op=ALU.mult
-            )
+            for cols in GPSIMD_PIECES:
+                nc.gpsimd.tensor_tensor(
+                    out=live["i", i][:, cols],
+                    in0=live["prop", i][:, cols],
+                    in1=live["i", i][:, cols],
+                    op=ALU.mult,
+                )
 
         def back(i, kind):
             g, c = divmod(i, GROUP)
@@ -355,12 +355,13 @@ def tile_relationalmemorycorecell_pa_t_kernel(
 
         def forget_times_m(i):
             g, c = divmod(i, GROUP)
-            nc.gpsimd.tensor_tensor(
-                out=live["f", i][:],
-                in0=live["m_again", g][:, c, :],
-                in1=live["f", i][:],
-                op=ALU.mult,
-            )
+            for cols in GPSIMD_PIECES:
+                nc.gpsimd.tensor_tensor(
+                    out=live["f", i][:, cols],
+                    in0=live["m", g][:, c, cols],
+                    in1=live["f", i][:, cols],
+                    op=ALU.mult,
+                )
 
         def kept_sigmoid(i):
             nc.scalar.activation(
@@ -386,10 +387,6 @@ def tile_relationalmemorycorecell_pa_t_kernel(
             )
             nc.sync.dma_start(out=out_0[batch, slot, :], in_=live["f", i][:])
 
-        def load_biases():
-            for j, bias in enumerate((b_ui, b_uo, b_g, b_uf)):
-                nc.scalar.dma_start(out=bias_rows[0:1, j, :], in_=bias.unsqueeze(0))
-
         def spread_biases():
             spread = psum.tile([P, WIDTH], F32, name="acc_f")
             nc.tensor.matmul(
@@ -410,6 +407,8 @@ def tile_relationalmemorycorecell_pa_t_kernel(
 
         bias_rows = consts.tile([P, 4, WIDTH], BF16, name="bias_rows")
         nc.vector.memset(bias_rows[:], 0.0)
+        for j, bias in enumerate((b_ui, b_uo, b_g, b_uf)):
+            nc.scalar.dma_start(out=bias_rows[0:1, j, :], in_=bias.unsqueeze(0))
         bias_f = consts.tile([P, WIDTH], F32, name="bias_f")
         bias_words = consts.tile([P, 3, 2], F32, name="bias_words")
         bias_col = consts.tile([P, 3 * BLOCKS], F32, name="bias_col")
@@ -418,6 +417,9 @@ def tile_relationalmemorycorecell_pa_t_kernel(
         ones = consts.tile([P, P], BF16, name="ones")
         nc.vector.memset(ones[:], 1.0)
 
+        for piece in range(W_FIRST):
+            load_weight(piece)
+
         for n in range(FIRST_STEP, STEPS + BACK_LAG + 1):
             multiplied = n if 0 <= n < STEPS else None
             along = due(n, -ALONG_LAG, 1, STEPS)
@@ -425,7 +427,7 @@ def tile_relationalmemorycorecell_pa_t_kernel(
             turning = due(n, TURN_LEAD, 1, STEPS)
 
             piece = due(n, W_LOAD_LEAD, 1, N_PIECES)
-            if piece is not None:
+            if piece is not None and piece >= W_FIRST:
                 load_weight(piece)
             half = due(n, X_LOAD_LEAD, STEPS_PER_HALF, HALVES)
             if half is not None:
@@ -436,11 +438,6 @@ def tile_relationalmemorycorecell_pa_t_kernel(
             g = due(n, M_LOAD_LEAD, GROUP, GROUPS)
             if g is not None:
                 load_m(g)
-            if n == BIAS_LOAD_STEP:
-                load_biases()
-            g = due(n, M_AGAIN_LEAD, GROUP, GROUPS)
-            if g is not None:
-                load_m_again(g)
 
             piece = due(n, W_REGROUP_LEAD, 1, N_PIECES)
             if piece is not None:

@@ -35,7 +35,7 @@ FLOPS = 2 * (4 * BATCH * SLOTS * WIDTH * WIDTH + 3 * BATCH * D_IN * WIDTH)
 
 W_UI, W_XI, W_UO, W_XO, W_G, W_XF, W_UF = 0, 1, 3, 4, 6, 7, 9
 N_PIECES = 10
-SCALAR_S_PIECE = 1
+S_PIECES = (4, 8)
 N_ACROSS = 7
 B_I, B_O, B_G = 0, 1, 2
 
@@ -43,24 +43,41 @@ LOAD_LEAD = 8
 TURN_LEAD = 5
 TANH_LEAD = 8
 ALONG_LAG = 2
-BACK_LAG = 5
-W_LOAD_LEAD, W_REGROUP_LEAD, W_QUANTISE_LEAD = 11, 8, 7
-X_LOAD_LEAD, X_TURN_LEAD, X_QUANTISE_LEAD = 9, 6, 4
+ALONG_LAST = 2
+KEPT_LAG = 4
+P_ON_VECTOR, F_ON_VECTOR = 1, 0
+BACK_LAG = 6
+W_STEPS = (-8, -7, -6, -5, -4, -3, -2, -1, 0, 1)
+X_LOAD_LEAD = 9
+X_TURN = (-6, STEPS_PER_HALF - 6)
+X_QUANTISE = (-4, STEPS_PER_HALF - 4)
 M_LOAD_LEAD = TANH_LEAD + GROUP
 BIAS_STEP = -3
-FIRST_STEP = -max(M_LOAD_LEAD, W_LOAD_LEAD)
+FIRST_STEP = -24
 
+GATE_TERMS = (ALONG_LAG - 1, STEPS_PER_HALF - 2)
+AT_F = tuple(
+    i + min(ALONG_LAG, max(ALONG_LAST, ALONG_LAST + GROUPS - 1 - i // GROUP)) for i in range(STEPS)
+)
+KEPT_AFTER = 2
+AT_KEPT = tuple(max(n + KEPT_AFTER, i + KEPT_LAG) for i, n in enumerate(AT_F))
 LOADED_BUFS = 4
-W_BUFS = 4
-W_FIRST = 2
+W_BUFS = 5
+FIRST_LOADS = ("w0", "x0", "m0", "w1", "w2", "w3", "h0", "w4")
+LOADS = {-7: ("w5", "m1"), -6: ("w6", "p0"), -5: ("w7", "h1"), -4: ("w8",), -3: ("w9", "p1"), -2: ("m2",)}
+MX_BUFS = {"h": 3, "p": 2}
 M_BUFS = 5
-ACROSS_BUFS = 2 * BLOCKS
+ACROSS_BUFS = BACK_LAG + BLOCKS
 PROP_BUFS = 3
-ALONG_BUFS = 5
+ALONG_BUFS = 6
 TANH_BUFS = TANH_LEAD + BACK_LAG + 1
 
 
 GPSIMD_PIECES = (slice(0, WIDTH // 2), slice(WIDTH // 2, WIDTH))
+
+
+def items(step, steps, shift=0):
+    return [i for i, at in enumerate(steps) if at + shift == step]
 
 
 def due(step, lead, every, count):
@@ -140,12 +157,17 @@ def tile_relationalmemorycorecell_pa_t_kernel(
             nc.sync.dma_start(out=m_rows[:], in_=m_state[batch, first : first + GROUP, :])
             live["m", g] = m_rows
 
-        def load_group(g):
+        def load_rows(kind, source, g):
             batch, first = where(g)
-            for kind, source in (("h", h_state), ("p", mem_att)):
-                loaded = work.tile([P, GROUP, WIDTH], BF16, name="loaded", bufs=LOADED_BUFS)
-                nc.sync.dma_start(out=loaded[:], in_=source[batch, first : first + GROUP, :])
-                live[kind, g] = loaded
+            loaded = work.tile([P, GROUP, WIDTH], BF16, name="loaded", bufs=LOADED_BUFS)
+            nc.sync.dma_start(out=loaded[:], in_=source[batch, first : first + GROUP, :])
+            live[kind, g] = loaded
+
+        def load_h(g):
+            load_rows("h", h_state, g)
+
+        def load_p(g):
+            load_rows("p", mem_att, g)
 
         def load_weight(piece):
             w_rows = work.tile([P, PACK, WIDTH], BF16, name="w_rows", bufs=W_BUFS)
@@ -161,17 +183,18 @@ def tile_relationalmemorycorecell_pa_t_kernel(
             live["x", half] = x_rows
 
         def regroup_weight(piece):
-            grouped = work.tile([P, WIDTH, PACK], BF16, name="w_grouped", align_bytes=64)
+            grouped = work.tile([P, WIDTH, PACK], BF16, name="w_grouped", align_bytes=64, bufs=3)
             if piece < N_ACROSS:
                 by_block = grouped[:].rearrange("q (u e j) t -> q u e j t", u=2, e=2)
                 by_column = live["w", piece][:].rearrange("q t (u j e) -> q u e j t", u=2, e=2)
-                if piece % 3 == SCALAR_S_PIECE:
+                if piece in S_PIECES:
                     for u in range(2):
                         nc.scalar.copy(out=by_block[:, u], in_=by_column[:, u])
                 else:
                     nc.vector.tensor_copy(out=by_block, in_=by_column)
             else:
-                nc.vector.tensor_copy(
+                copy = nc.scalar.copy if piece in S_PIECES else nc.vector.tensor_copy
+                copy(
                     out=grouped[:].rearrange("q (c i) t -> q c t i", i=4),
                     in_=live["w", piece][:].rearrange("q t (c i) -> q c t i", i=4),
                 )
@@ -216,7 +239,7 @@ def tile_relationalmemorycorecell_pa_t_kernel(
             return x_words[:, half, a, 0:columns], x_scales[:, half, a, 0:columns]
 
         def gate_terms(half):
-            acc = psum.tile([P, WIDTH], F32, name="acc_f")
+            acc = psum.tile([P, WIDTH], F32, name="turned", bufs=2)
             for a in range(X_PASSES):
                 mx(acc[:], x_operand(half, a, P), weight(W_XF + a), a == 0, a == X_PASSES - 1)
             nc.vector.tensor_add(out=gate_add[:, half, :], in0=acc[:], in1=bias_f[:])
@@ -248,8 +271,9 @@ def tile_relationalmemorycorecell_pa_t_kernel(
             )
 
         def quantise(kind, g):
-            words = work.tile([P, ROWS], U32, name=kind + "_words", align_bytes=64)
-            scales = work.tile([P, ROWS], U8, name=kind + "_scales", align_bytes=64)
+            bufs = MX_BUFS[kind]
+            words = work.tile([P, ROWS], U32, name=kind + "_words", align_bytes=64, bufs=bufs)
+            scales = work.tile([P, ROWS], U8, name=kind + "_scales", align_bytes=64, bufs=bufs)
             nc.vector.quantize_mx(
                 out=words[:].bitcast(FP8X4),
                 scales=scales[:],
@@ -311,8 +335,9 @@ def tile_relationalmemorycorecell_pa_t_kernel(
             live["prop", i] = prop
 
         def prop_times_gate(i):
+            engine = nc.vector if i >= STEPS - P_ON_VECTOR else nc.gpsimd
             for cols in GPSIMD_PIECES:
-                nc.gpsimd.tensor_tensor(
+                engine.tensor_tensor(
                     out=live["i", i][:, cols],
                     in0=live["prop", i][:, cols],
                     in1=live["i", i][:, cols],
@@ -321,7 +346,10 @@ def tile_relationalmemorycorecell_pa_t_kernel(
 
         def back(i, kind):
             g, c = divmod(i, GROUP)
-            bank = psum.tile([P, BLOCKS, P], F32, name="back_" + kind)
+            name = "back_" + kind
+            if g == GROUPS - 1 and c % 2:
+                name = {"o": "acc_o", "i": "acc_i"}[kind]
+            bank = psum.tile([P, BLOCKS, P], F32, name=name)
             for t in range(BLOCKS):
                 nc.tensor.transpose(
                     bank[:, t, :], live[kind, g * BLOCKS + t][:, c * P : (c + 1) * P], ident[:]
@@ -355,8 +383,9 @@ def tile_relationalmemorycorecell_pa_t_kernel(
 
         def forget_times_m(i):
             g, c = divmod(i, GROUP)
+            engine = nc.vector if i >= STEPS - F_ON_VECTOR else nc.gpsimd
             for cols in GPSIMD_PIECES:
-                nc.gpsimd.tensor_tensor(
+                engine.tensor_tensor(
                     out=live["f", i][:, cols],
                     in0=live["m", g][:, c, cols],
                     in1=live["f", i][:, cols],
@@ -405,8 +434,12 @@ def tile_relationalmemorycorecell_pa_t_kernel(
                 out=bias_col[:], in_=bias_words[:].rearrange("q g u -> q (g u)").bitcast(BF16)
             )
 
+        ones = consts.tile([P, P], BF16, name="ones")
+        nc.vector.memset(ones[:], 1.0)
+        warm = consts.tile([P, 1], F32, name="warm")
+        nc.scalar.activation(out=warm[:], in_=ones[:, 0:1], func=FUNC.Sigmoid)
         bias_rows = consts.tile([P, 4, WIDTH], BF16, name="bias_rows")
-        nc.vector.memset(bias_rows[:], 0.0)
+        nc.vector.memset(bias_rows[:].bitcast(F32), 0.0)
         for j, bias in enumerate((b_ui, b_uo, b_g, b_uf)):
             nc.scalar.dma_start(out=bias_rows[0:1, j, :], in_=bias.unsqueeze(0))
         bias_f = consts.tile([P, WIDTH], F32, name="bias_f")
@@ -414,72 +447,47 @@ def tile_relationalmemorycorecell_pa_t_kernel(
         bias_col = consts.tile([P, 3 * BLOCKS], F32, name="bias_col")
         ident = consts.tile([P, P], F32, name="ident")
         make_identity(nc, ident[:])
-        ones = consts.tile([P, P], BF16, name="ones")
-        nc.vector.memset(ones[:], 1.0)
 
-        for piece in range(W_FIRST):
-            load_weight(piece)
+        loaders = {"w": load_weight, "x": load_x, "m": load_m, "h": load_h, "p": load_p}
+        for item in FIRST_LOADS:
+            loaders[item[0]](int(item[1:]))
+
+        def load(kind, number):
+            if number is not None and kind + str(number) not in FIRST_LOADS + sum(LOADS.values(), ()):
+                loaders[kind](number)
 
         for n in range(FIRST_STEP, STEPS + BACK_LAG + 1):
             multiplied = n if 0 <= n < STEPS else None
-            along = due(n, -ALONG_LAG, 1, STEPS)
             finished = due(n, -BACK_LAG, 1, STEPS)
             turning = due(n, TURN_LEAD, 1, STEPS)
 
-            piece = due(n, W_LOAD_LEAD, 1, N_PIECES)
-            if piece is not None and piece >= W_FIRST:
-                load_weight(piece)
-            half = due(n, X_LOAD_LEAD, STEPS_PER_HALF, HALVES)
-            if half is not None:
-                load_x(half)
-            g = due(n, LOAD_LEAD, GROUP, GROUPS)
-            if g is not None:
-                load_group(g)
-            g = due(n, M_LOAD_LEAD, GROUP, GROUPS)
-            if g is not None:
-                load_m(g)
+            for item in LOADS.get(n, ()):
+                loaders[item[0]](int(item[1:]))
+            load("x", due(n, X_LOAD_LEAD, STEPS_PER_HALF, HALVES))
+            load("h", due(n, LOAD_LEAD, GROUP, GROUPS))
+            load("p", due(n, LOAD_LEAD - 1, GROUP, GROUPS))
+            load("m", due(n, M_LOAD_LEAD, GROUP, GROUPS))
 
-            piece = due(n, W_REGROUP_LEAD, 1, N_PIECES)
-            if piece is not None:
+            for piece in items(n, W_STEPS):
                 regroup_weight(piece)
-            piece = due(n, W_QUANTISE_LEAD, 1, N_PIECES)
-            if piece is not None:
+            for piece in items(n, W_STEPS, 1):
                 quantise_weight(piece)
 
+            early = items(n, AT_F)[: -1 if n < STEPS else None]
+            for i in early:
+                forget_product(i)
+                forget_sum(i)
             if finished is not None:
                 back(finished, "o")
                 back(finished, "i")
-            if turning is not None:
-                turn(turning)
-            half = due(n, X_TURN_LEAD, STEPS_PER_HALF, HALVES)
-            if half is not None:
+            for half in items(n, X_TURN):
                 turn_x(half)
             if n == BIAS_STEP:
                 spread_biases()
             if finished is not None:
                 finish(finished)
-            if turning is not None:
-                regroup(turning)
-            half = due(n, X_QUANTISE_LEAD, STEPS_PER_HALF, HALVES)
-            if half is not None:
+            for half in items(n, X_QUANTISE):
                 quantise_x(half)
-
-            if multiplied is not None:
-                gate_across(n, "i", W_UI, W_XI)
-                gate_across(n, "o", W_UO, W_XO)
-                prop_across(n)
-            half = due(n, -(ALONG_LAG - 1), STEPS_PER_HALF, HALVES)
-            if half is not None:
-                gate_terms(half)
-            if along is not None:
-                forget_product(along)
-
-            if multiplied is not None:
-                first_sigmoid(n, "i", B_I)
-                first_sigmoid(n, "o", B_O)
-                prop_sum(n)
-            if along is not None:
-                forget_sum(along)
             g = due(n, TURN_LEAD - 2, GROUP, GROUPS)
             if g is not None:
                 quantise("h", g)
@@ -487,17 +495,36 @@ def tile_relationalmemorycorecell_pa_t_kernel(
             if g is not None:
                 quantise("p", g)
 
-            if due(n, -(ALONG_LAG + 1), 1, STEPS) is not None:
-                forget_sigmoid(n - ALONG_LAG - 1)
+            if multiplied is not None:
+                gate_across(n, "i", W_UI, W_XI)
+                gate_across(n, "o", W_UO, W_XO)
+                prop_across(n)
+            for half in items(n, GATE_TERMS):
+                gate_terms(half)
+            for i in items(n, AT_F)[len(early) :]:
+                forget_product(i)
+
+            if multiplied is not None:
+                first_sigmoid(n, "i", B_I)
+                first_sigmoid(n, "o", B_O)
+                prop_sum(n)
+            for i in items(n, AT_F)[len(early) :]:
+                forget_sum(i)
+            if turning is not None:
+                turn(turning)
+                regroup(turning)
+
+            for i in items(n, AT_F, 1):
+                forget_sigmoid(i)
             if multiplied is not None:
                 second_sigmoid(n, "i")
                 second_sigmoid(n, "o")
-            if due(n, -(ALONG_LAG + 2), 1, STEPS) is not None:
-                kept_sigmoid(n - ALONG_LAG - 2)
+            for i in items(n, AT_KEPT):
+                kept_sigmoid(i)
             if due(n, TANH_LEAD, 1, STEPS) is not None:
                 tanh_of_m(n + TANH_LEAD)
 
             if due(n, -1, 1, STEPS) is not None:
                 prop_times_gate(n - 1)
-            if due(n, -(ALONG_LAG + 1), 1, STEPS) is not None:
-                forget_times_m(n - ALONG_LAG - 1)
+            for i in items(n, AT_F, 1):
+                forget_times_m(i)

@@ -41,39 +41,40 @@ B_I, B_O, B_G = 0, 1, 2
 
 LOAD_LEAD = 8
 TURN_LEAD = 5
-TANH_LEAD = 8
+TANH_LEAD = 12
 ALONG_LAG = 2
-ALONG_LAST = 2
+LAST_F = STEPS + 1
+LAST_KEPT = STEPS + 3
 KEPT_LAG = 4
 P_ON_VECTOR, F_ON_VECTOR = 1, 0
+CATCH_UP = 0
 BACK_LAG = 6
 W_STEPS = (-8, -7, -6, -5, -4, -3, -2, -1, 0, 1)
 X_LOAD_LEAD = 9
 X_TURN = (-6, STEPS_PER_HALF - 6)
 X_QUANTISE = (-4, STEPS_PER_HALF - 4)
 M_LOAD_LEAD = TANH_LEAD + GROUP
-BIAS_STEP = -3
+BIAS_STEP = -7
 FIRST_STEP = -24
 
-GATE_TERMS = (ALONG_LAG - 1, STEPS_PER_HALF - 2)
-AT_F = tuple(
-    i + min(ALONG_LAG, max(ALONG_LAST, ALONG_LAST + GROUPS - 1 - i // GROUP)) for i in range(STEPS)
-)
+GATE_TERMS = (ALONG_LAG, STEPS_PER_HALF - 2)
+AT_BACK = tuple(i + BACK_LAG + (i < CATCH_UP) for i in range(STEPS))
+AT_F = tuple(i + ALONG_LAG + (i < CATCH_UP) for i in range(STEPS))
 KEPT_AFTER = 2
-AT_KEPT = tuple(max(n + KEPT_AFTER, i + KEPT_LAG) for i, n in enumerate(AT_F))
-LOADED_BUFS = 4
+AT_KEPT = tuple(n + KEPT_AFTER for n in AT_F)
+LOADED_BUFS = 3
 W_BUFS = 5
-FIRST_LOADS = ("w0", "x0", "m0", "w1", "w2", "w3", "h0", "w4")
-LOADS = {-7: ("w5", "m1"), -6: ("w6", "p0"), -5: ("w7", "h1"), -4: ("w8",), -3: ("w9", "p1"), -2: ("m2",)}
+FIRST_LOADS = ("w0", "x0", "m0", "w1", "w2", "m1", "w3", "h0", "w4")
+LOADS = {-7: ("w5", "m2"), -6: ("w6", "p0"), -5: ("w7", "h1"), -4: ("w8",), -3: ("w9", "p1")}
 MX_BUFS = {"h": 3, "p": 2}
-M_BUFS = 5
-ACROSS_BUFS = BACK_LAG + BLOCKS
+M_BUFS = 6
+ACROSS_BUFS = BACK_LAG + BLOCKS - 1
 PROP_BUFS = 3
 ALONG_BUFS = 6
 TANH_BUFS = TANH_LEAD + BACK_LAG + 1
 
 
-GPSIMD_PIECES = (slice(0, WIDTH // 2), slice(WIDTH // 2, WIDTH))
+GPSIMD_PIECES = (slice(0, WIDTH),)
 
 
 def items(step, steps, shift=0):
@@ -438,7 +439,7 @@ def tile_relationalmemorycorecell_pa_t_kernel(
         nc.vector.memset(ones[:], 1.0)
         warm = consts.tile([P, 1], F32, name="warm")
         nc.scalar.activation(out=warm[:], in_=ones[:, 0:1], func=FUNC.Sigmoid)
-        bias_rows = consts.tile([P, 4, WIDTH], BF16, name="bias_rows")
+        bias_rows = work.tile([P, 4, WIDTH], BF16, name="loaded", bufs=LOADED_BUFS)
         nc.vector.memset(bias_rows[:].bitcast(F32), 0.0)
         for j, bias in enumerate((b_ui, b_uo, b_g, b_uf)):
             nc.scalar.dma_start(out=bias_rows[0:1, j, :], in_=bias.unsqueeze(0))
@@ -458,7 +459,7 @@ def tile_relationalmemorycorecell_pa_t_kernel(
 
         for n in range(FIRST_STEP, STEPS + BACK_LAG + 1):
             multiplied = n if 0 <= n < STEPS else None
-            finished = due(n, -BACK_LAG, 1, STEPS)
+            finished = items(n, AT_BACK)
             turning = due(n, TURN_LEAD, 1, STEPS)
 
             for item in LOADS.get(n, ()):
@@ -477,15 +478,19 @@ def tile_relationalmemorycorecell_pa_t_kernel(
             for i in early:
                 forget_product(i)
                 forget_sum(i)
-            if finished is not None:
-                back(finished, "o")
-                back(finished, "i")
+            for i in finished[:1]:
+                back(i, "o")
+                back(i, "i")
             for half in items(n, X_TURN):
                 turn_x(half)
             if n == BIAS_STEP:
                 spread_biases()
-            if finished is not None:
-                finish(finished)
+            for i in finished[:1]:
+                finish(i)
+            for i in finished[1:]:
+                back(i, "o")
+                back(i, "i")
+                finish(i)
             for half in items(n, X_QUANTISE):
                 quantise_x(half)
             g = due(n, TURN_LEAD - 2, GROUP, GROUPS)

@@ -192,7 +192,12 @@ def tile_relationalmemorycorecell_pa_t_kernel(
                     for u in range(2):
                         nc.scalar.copy(out=by_block[:, u], in_=by_column[:, u])
                 else:
-                    nc.vector.tensor_copy(out=by_block, in_=by_column)
+                    by_block = grouped[:].rearrange("q (u e k i) t -> q u k t i e", u=2, e=2, i=2)
+                    by_column = live["w", piece][:].rearrange(
+                        "q t (u k i e) -> q u k t i e", u=2, i=2, e=2
+                    )
+                    for u in range(2):
+                        nc.vector.tensor_copy(out=by_block[:, u], in_=by_column[:, u])
             else:
                 copy = nc.scalar.copy if piece in S_PIECES else nc.vector.tensor_copy
                 copy(

@@ -35,37 +35,25 @@ FLOPS = 2 * (4 * BATCH * SLOTS * WIDTH * WIDTH + 3 * BATCH * D_IN * WIDTH)
 
 W_UI, W_XI, W_UO, W_XO, W_G, W_XF, W_UF = 0, 1, 3, 4, 6, 7, 9
 N_PIECES = 10
-S_PIECES = (4, 8)
 N_ACROSS = 7
+SCALAR_EVERY = 4
 B_I, B_O, B_G = 0, 1, 2
 
-LOAD_LEAD = 8
 TURN_LEAD = 5
+X_TURN_LEAD, X_QUANTISE_LEAD = 6, 4
 TANH_LEAD = 12
 ALONG_LAG = 2
-LAST_F = STEPS + 1
-LAST_KEPT = STEPS + 3
-KEPT_LAG = 4
-P_ON_VECTOR, F_ON_VECTOR = 1, 0
-CATCH_UP = 0
-BACK_LAG = 6
-W_STEPS = (-8, -7, -6, -5, -4, -3, -2, -1, 0, 1)
-X_LOAD_LEAD = 9
-X_TURN = (-6, STEPS_PER_HALF - 6)
-X_QUANTISE = (-4, STEPS_PER_HALF - 4)
-M_LOAD_LEAD = TANH_LEAD + GROUP
-BIAS_STEP = -7
-FIRST_STEP = -24
+KEPT_LAG = ALONG_LAG + 2
+BACK_LAG = KEPT_LAG + 2
+W_LEAD = N_PIECES - ALONG_LAG
+BIAS_STEP = 1 - W_LEAD
+LOAD_LEAD = 4
+M_LOAD_LEAD = TANH_LEAD + 2
+FIRST_STEP = -M_LOAD_LEAD
 
-GATE_TERMS = (ALONG_LAG, STEPS_PER_HALF - 2)
-AT_BACK = tuple(i + BACK_LAG + (i < CATCH_UP) for i in range(STEPS))
-AT_F = tuple(i + ALONG_LAG + (i < CATCH_UP) for i in range(STEPS))
-KEPT_AFTER = 2
-AT_KEPT = tuple(n + KEPT_AFTER for n in AT_F)
 LOADED_BUFS = 3
-W_BUFS = 5
-FIRST_LOADS = ("w0", "x0", "m0", "w1", "w2", "m1", "w3", "h0", "w4")
-LOADS = {-7: ("w5", "m2"), -6: ("w6", "p0"), -5: ("w7", "h1"), -4: ("w8",), -3: ("w9", "p1")}
+W_BUFS = LOAD_LEAD + 1
+W_GROUPED_BUFS = 3
 MX_BUFS = {"h": 3, "p": 2}
 M_BUFS = 6
 ACROSS_BUFS = BACK_LAG + BLOCKS - 1
@@ -74,16 +62,25 @@ ALONG_BUFS = 6
 TANH_BUFS = TANH_LEAD + BACK_LAG + 1
 
 
-GPSIMD_PIECES = (slice(0, WIDTH),)
+def due(n, lead, every, count):
+    item, rest = divmod(n + lead, every)
+    return (item,) if rest == 0 and 0 <= item < count else ()
 
 
-def items(step, steps, shift=0):
-    return [i for i, at in enumerate(steps) if at + shift == step]
+def of_slot(n, lead):
+    return due(n, lead, 1, STEPS)
 
 
-def due(step, lead, every, count):
-    number, rest = divmod(step + lead, every)
-    return number if rest == 0 and 0 <= number < count else None
+def of_group(n, lead):
+    return due(n, lead, GROUP, GROUPS)
+
+
+def of_half(n, lead):
+    return due(n, lead, STEPS_PER_HALF, HALVES)
+
+
+def of_weight(n, lead):
+    return due(n, lead, 1, N_PIECES)
 
 
 def tile_relationalmemorycorecell_pa_t_kernel(
@@ -164,12 +161,6 @@ def tile_relationalmemorycorecell_pa_t_kernel(
             nc.sync.dma_start(out=loaded[:], in_=source[batch, first : first + GROUP, :])
             live[kind, g] = loaded
 
-        def load_h(g):
-            load_rows("h", h_state, g)
-
-        def load_p(g):
-            load_rows("p", mem_att, g)
-
         def load_weight(piece):
             w_rows = work.tile([P, PACK, WIDTH], BF16, name="w_rows", bufs=W_BUFS)
             nc.sync.dma_start(
@@ -184,26 +175,27 @@ def tile_relationalmemorycorecell_pa_t_kernel(
             live["x", half] = x_rows
 
         def regroup_weight(piece):
-            grouped = work.tile([P, WIDTH, PACK], BF16, name="w_grouped", align_bytes=64, bufs=3)
-            if piece < N_ACROSS:
-                by_block = grouped[:].rearrange("q (u e j) t -> q u e j t", u=2, e=2)
-                by_column = live["w", piece][:].rearrange("q t (u j e) -> q u e j t", u=2, e=2)
-                if piece in S_PIECES:
-                    for u in range(2):
-                        nc.scalar.copy(out=by_block[:, u], in_=by_column[:, u])
-                else:
-                    by_block = grouped[:].rearrange("q (u e k i) t -> q u k t i e", u=2, e=2, i=2)
-                    by_column = live["w", piece][:].rearrange(
-                        "q t (u k i e) -> q u k t i e", u=2, i=2, e=2
-                    )
-                    for u in range(2):
-                        nc.vector.tensor_copy(out=by_block[:, u], in_=by_column[:, u])
-            else:
-                copy = nc.scalar.copy if piece in S_PIECES else nc.vector.tensor_copy
+            grouped = work.tile(
+                [P, WIDTH, PACK], BF16, name="w_grouped", align_bytes=64, bufs=W_GROUPED_BUFS
+            )
+            rows = live["w", piece]
+            by_scalar = piece > 0 and piece % SCALAR_EVERY == 0
+            copy = nc.scalar.copy if by_scalar else nc.vector.tensor_copy
+            if piece >= N_ACROSS:
                 copy(
                     out=grouped[:].rearrange("q (c i) t -> q c t i", i=4),
-                    in_=live["w", piece][:].rearrange("q t (c i) -> q c t i", i=4),
+                    in_=rows[:].rearrange("q t (c i) -> q c t i", i=4),
                 )
+            elif by_scalar:
+                out = grouped[:].rearrange("q (u e j) t -> q u e j t", u=2, e=2)
+                columns = rows[:].rearrange("q t (u j e) -> q u e j t", u=2, e=2)
+                for u in range(2):
+                    copy(out=out[:, u], in_=columns[:, u])
+            else:
+                out = grouped[:].rearrange("q (u e k i) t -> q u k t i e", u=2, e=2, i=2)
+                columns = rows[:].rearrange("q t (u k i e) -> q u k t i e", u=2, i=2, e=2)
+                for u in range(2):
+                    copy(out=out[:, u], in_=columns[:, u])
             live["w_grouped", piece] = grouped
 
         def quantise_weight(piece):
@@ -341,21 +333,15 @@ def tile_relationalmemorycorecell_pa_t_kernel(
             live["prop", i] = prop
 
         def prop_times_gate(i):
-            engine = nc.vector if i >= STEPS - P_ON_VECTOR else nc.gpsimd
-            for cols in GPSIMD_PIECES:
-                engine.tensor_tensor(
-                    out=live["i", i][:, cols],
-                    in0=live["prop", i][:, cols],
-                    in1=live["i", i][:, cols],
-                    op=ALU.mult,
-                )
+            engine = nc.vector if i == STEPS - 1 else nc.gpsimd
+            engine.tensor_tensor(
+                out=live["i", i][:], in0=live["prop", i][:], in1=live["i", i][:], op=ALU.mult
+            )
 
         def back(i, kind):
             g, c = divmod(i, GROUP)
-            name = "back_" + kind
-            if g == GROUPS - 1 and c % 2:
-                name = {"o": "acc_o", "i": "acc_i"}[kind]
-            bank = psum.tile([P, BLOCKS, P], F32, name=name)
+            role = "acc_" if g == GROUPS - 1 and c % 2 else "back_"
+            bank = psum.tile([P, BLOCKS, P], F32, name=role + kind)
             for t in range(BLOCKS):
                 nc.tensor.transpose(
                     bank[:, t, :], live[kind, g * BLOCKS + t][:, c * P : (c + 1) * P], ident[:]
@@ -389,14 +375,9 @@ def tile_relationalmemorycorecell_pa_t_kernel(
 
         def forget_times_m(i):
             g, c = divmod(i, GROUP)
-            engine = nc.vector if i >= STEPS - F_ON_VECTOR else nc.gpsimd
-            for cols in GPSIMD_PIECES:
-                engine.tensor_tensor(
-                    out=live["f", i][:, cols],
-                    in0=live["m", g][:, c, cols],
-                    in1=live["f", i][:, cols],
-                    op=ALU.mult,
-                )
+            nc.gpsimd.tensor_tensor(
+                out=live["f", i][:], in0=live["m", g][:, c, :], in1=live["f", i][:], op=ALU.mult
+            )
 
         def kept_sigmoid(i):
             nc.scalar.activation(
@@ -454,87 +435,74 @@ def tile_relationalmemorycorecell_pa_t_kernel(
         ident = consts.tile([P, P], F32, name="ident")
         make_identity(nc, ident[:])
 
-        loaders = {"w": load_weight, "x": load_x, "m": load_m, "h": load_h, "p": load_p}
-        for item in FIRST_LOADS:
-            loaders[item[0]](int(item[1:]))
-
-        def load(kind, number):
-            if number is not None and kind + str(number) not in FIRST_LOADS + sum(LOADS.values(), ()):
-                loaders[kind](number)
 
         for n in range(FIRST_STEP, STEPS + BACK_LAG + 1):
-            multiplied = n if 0 <= n < STEPS else None
-            finished = items(n, AT_BACK)
-            turning = due(n, TURN_LEAD, 1, STEPS)
+            for piece in of_weight(n, W_LEAD + LOAD_LEAD):
+                load_weight(piece)
+            for half in of_half(n, X_TURN_LEAD + LOAD_LEAD):
+                load_x(half)
+            for g in of_group(n, M_LOAD_LEAD):
+                load_m(g)
+            for g in of_group(n, TURN_LEAD + LOAD_LEAD):
+                load_rows("h", h_state, g)
+            for g in of_group(n, TURN_LEAD + LOAD_LEAD - 2):
+                load_rows("p", mem_att, g)
 
-            for item in LOADS.get(n, ()):
-                loaders[item[0]](int(item[1:]))
-            load("x", due(n, X_LOAD_LEAD, STEPS_PER_HALF, HALVES))
-            load("h", due(n, LOAD_LEAD, GROUP, GROUPS))
-            load("p", due(n, LOAD_LEAD - 1, GROUP, GROUPS))
-            load("m", due(n, M_LOAD_LEAD, GROUP, GROUPS))
-
-            for piece in items(n, W_STEPS):
+            for piece in of_weight(n, W_LEAD):
                 regroup_weight(piece)
-            for piece in items(n, W_STEPS, 1):
+            for piece in of_weight(n, W_LEAD - 1):
                 quantise_weight(piece)
 
-            early = items(n, AT_F)[: -1 if n < STEPS else None]
-            for i in early:
-                forget_product(i)
-                forget_sum(i)
-            for i in finished[:1]:
+            if n >= STEPS:
+                for i in of_slot(n, -ALONG_LAG):
+                    forget_product(i)
+                    forget_sum(i)
+            for i in of_slot(n, -BACK_LAG):
                 back(i, "o")
                 back(i, "i")
-            for half in items(n, X_TURN):
+            for half in of_half(n, X_TURN_LEAD):
                 turn_x(half)
             if n == BIAS_STEP:
                 spread_biases()
-            for i in finished[:1]:
+            for i in of_slot(n, -BACK_LAG):
                 finish(i)
-            for i in finished[1:]:
-                back(i, "o")
-                back(i, "i")
-                finish(i)
-            for half in items(n, X_QUANTISE):
+            for half in of_half(n, X_QUANTISE_LEAD):
                 quantise_x(half)
-            g = due(n, TURN_LEAD - 2, GROUP, GROUPS)
-            if g is not None:
+            for g in of_group(n, TURN_LEAD - 2):
                 quantise("h", g)
-            g = due(n, TURN_LEAD - 4, GROUP, GROUPS)
-            if g is not None:
+            for g in of_group(n, TURN_LEAD - 4):
                 quantise("p", g)
 
-            if multiplied is not None:
-                gate_across(n, "i", W_UI, W_XI)
-                gate_across(n, "o", W_UO, W_XO)
-                prop_across(n)
-            for half in items(n, GATE_TERMS):
+            for i in of_slot(n, 0):
+                gate_across(i, "i", W_UI, W_XI)
+                gate_across(i, "o", W_UO, W_XO)
+                prop_across(i)
+            for half in of_half(n, -ALONG_LAG):
                 gate_terms(half)
-            for i in items(n, AT_F)[len(early) :]:
-                forget_product(i)
+            if n < STEPS:
+                for i in of_slot(n, -ALONG_LAG):
+                    forget_product(i)
+            for i in of_slot(n, 0):
+                first_sigmoid(i, "i", B_I)
+                first_sigmoid(i, "o", B_O)
+                prop_sum(i)
+            if n < STEPS:
+                for i in of_slot(n, -ALONG_LAG):
+                    forget_sum(i)
+            for w in of_slot(n, TURN_LEAD):
+                turn(w)
+                regroup(w)
 
-            if multiplied is not None:
-                first_sigmoid(n, "i", B_I)
-                first_sigmoid(n, "o", B_O)
-                prop_sum(n)
-            for i in items(n, AT_F)[len(early) :]:
-                forget_sum(i)
-            if turning is not None:
-                turn(turning)
-                regroup(turning)
-
-            for i in items(n, AT_F, 1):
+            for i in of_slot(n, -ALONG_LAG - 1):
                 forget_sigmoid(i)
-            if multiplied is not None:
-                second_sigmoid(n, "i")
-                second_sigmoid(n, "o")
-            for i in items(n, AT_KEPT):
+            for i in of_slot(n, 0):
+                second_sigmoid(i, "i")
+                second_sigmoid(i, "o")
+            for i in of_slot(n, -KEPT_LAG):
                 kept_sigmoid(i)
-            if due(n, TANH_LEAD, 1, STEPS) is not None:
-                tanh_of_m(n + TANH_LEAD)
-
-            if due(n, -1, 1, STEPS) is not None:
-                prop_times_gate(n - 1)
-            for i in items(n, AT_F, 1):
+            for i in of_slot(n, TANH_LEAD):
+                tanh_of_m(i)
+            for i in of_slot(n, -1):
+                prop_times_gate(i)
+            for i in of_slot(n, -ALONG_LAG - 1):
                 forget_times_m(i)

from contextlib import ExitStack

import concourse.mybir as mybir
from concourse.masks import make_identity

F32 = mybir.dt.float32
BF16 = mybir.dt.bfloat16
U32 = mybir.dt.uint32
U8 = mybir.dt.uint8
FP8X4 = mybir.dt.float8_e4m3fn_x4
FUNC = mybir.ActivationFunctionType
ALU = mybir.AluOpType

P = 128
BATCH = 256
SLOTS = 16
WIDTH = 512
D_IN = 1024
PACK = 4
K_PASS = P * PACK
HALVES = BATCH // P
X_PASSES = D_IN // K_PASS
GROUP = 4
ROWS = GROUP * P
BLOCKS = WIDTH // P
assert BLOCKS == GROUP
GROUPS_PER_HALF = SLOTS // GROUP
GROUPS = HALVES * GROUPS_PER_HALF
STEPS = GROUPS * GROUP
STEPS_PER_HALF = STEPS // HALVES

FORGET_BIAS = 1.0

FLOPS = 2 * (4 * BATCH * SLOTS * WIDTH * WIDTH + 3 * BATCH * D_IN * WIDTH)

W_UI, W_XI, W_UO, W_XO, W_G, W_XF, W_UF = 0, 1, 3, 4, 6, 7, 9
N_PIECES = 10
N_ACROSS = 7
SCALAR_EVERY = 4
B_I, B_O, B_G = 0, 1, 2

TURN_LEAD = 5
X_TURN_LEAD, X_QUANTISE_LEAD = 6, 4
TANH_LEAD = 12
ALONG_LAG = 2
KEPT_LAG = ALONG_LAG + 2
BACK_LAG = KEPT_LAG + 2
W_LEAD = N_PIECES - ALONG_LAG
BIAS_STEP = 1 - W_LEAD
LOAD_LEAD = 4
M_LOAD_LEAD = TANH_LEAD + 2
FIRST_STEP = -M_LOAD_LEAD

LOADED_BUFS = 3
W_BUFS = LOAD_LEAD + 1
W_GROUPED_BUFS = 3
MX_BUFS = {"h": 3, "p": 2}
M_BUFS = 6
ACROSS_BUFS = BACK_LAG + BLOCKS - 1
PROP_BUFS = 3
ALONG_BUFS = 6
TANH_BUFS = TANH_LEAD + BACK_LAG + 1


def due(n, lead, every, count):
    item, rest = divmod(n + lead, every)
    return (item,) if rest == 0 and 0 <= item < count else ()


def of_slot(n, lead):
    return due(n, lead, 1, STEPS)


def of_group(n, lead):
    return due(n, lead, GROUP, GROUPS)


def of_half(n, lead):
    return due(n, lead, STEPS_PER_HALF, HALVES)


def of_weight(n, lead):
    return due(n, lead, 1, N_PIECES)


def tile_relationalmemorycorecell_pa_t_kernel(
    tc,
    inputs,
    h_state,
    m_state,
    mem_att,
    W_g,
    b_g,
    W_wf,
    W_wi,
    W_wo,
    W_uf,
    b_uf,
    W_ui,
    b_ui,
    W_uo,
    b_uo,
    out_0,
    out_1,
):
    nc = tc.nc
    weight_pieces = (
        W_ui,
        W_wi[0:K_PASS, :],
        W_wi[K_PASS:D_IN, :],
        W_uo,
        W_wo[0:K_PASS, :],
        W_wo[K_PASS:D_IN, :],
        W_g,
        W_wf[0:K_PASS, :],
        W_wf[K_PASS:D_IN, :],
        W_uf,
    )
    with ExitStack() as pools:
        pools.enter_context(tc.manual_schedule())
        consts = pools.enter_context(tc.tile_pool(name="consts", bufs=1))
        work = pools.enter_context(tc.tile_pool(name="work", bufs=2))
        psum = pools.enter_context(tc.psum_pool(name="psum", bufs=1))

        live = {}

        w_words = consts.tile([P, N_PIECES, WIDTH], U32, name="w_words", align_bytes=64)
        w_scales = consts.tile([P, N_PIECES, WIDTH], U8, name="w_scales", align_bytes=64)
        x_words = consts.tile([P, HALVES, X_PASSES, ROWS], U32, name="x_words", align_bytes=64)
        x_scales = consts.tile([P, HALVES, X_PASSES, ROWS], U8, name="x_scales", align_bytes=64)
        gate_add = consts.tile([P, HALVES, WIDTH], F32, name="gate_add")

        def where(g):
            half, quarter = divmod(g, GROUPS_PER_HALF)
            return slice(half * P, (half + 1) * P), quarter * GROUP

        def mx(acc, stationary, moving, start, stop):
            nc.tensor.matmul_mx(
                out=acc,
                lhsT=stationary[0].bitcast(FP8X4),
                lhsT_scale=stationary[1],
                rhs=moving[0].bitcast(FP8X4),
                rhs_scale=moving[1],
                start=start,
                stop=stop,
            )

        def weight(piece, first=0, columns=WIDTH):
            cols = slice(first, first + columns)
            return w_words[:, piece, cols], w_scales[:, piece, cols]

        def load_m(g):
            batch, first = where(g)
            m_rows = work.tile([P, GROUP, WIDTH], BF16, name="m_rows", bufs=M_BUFS)
            nc.sync.dma_start(out=m_rows[:], in_=m_state[batch, first : first + GROUP, :])
            live["m", g] = m_rows

        def load_rows(kind, source, g):
            batch, first = where(g)
            loaded = work.tile([P, GROUP, WIDTH], BF16, name="loaded", bufs=LOADED_BUFS)
            nc.sync.dma_start(out=loaded[:], in_=source[batch, first : first + GROUP, :])
            live[kind, g] = loaded

        def load_weight(piece):
            w_rows = work.tile([P, PACK, WIDTH], BF16, name="w_rows", bufs=W_BUFS)
            nc.sync.dma_start(
                out=w_rows[:].rearrange("q (u e) n -> q u e n", u=2),
                in_=weight_pieces[piece].rearrange("(u q e) n -> q u e n", u=2, e=2),
            )
            live["w", piece] = w_rows

        def load_x(half):
            x_rows = work.tile([P, D_IN], BF16, name="x_rows", bufs=1)
            nc.sync.dma_start(out=x_rows[:], in_=inputs[half * P : (half + 1) * P, :])
            live["x", half] = x_rows

        def regroup_weight(piece):
            grouped = work.tile(
                [P, WIDTH, PACK], BF16, name="w_grouped", align_bytes=64, bufs=W_GROUPED_BUFS
            )
            rows = live["w", piece]
            by_scalar = piece > 0 and piece % SCALAR_EVERY == 0
            copy = nc.scalar.copy if by_scalar else nc.vector.tensor_copy
            if piece >= N_ACROSS:
                copy(
                    out=grouped[:].rearrange("q (c i) t -> q c t i", i=4),
                    in_=rows[:].rearrange("q t (c i) -> q c t i", i=4),
                )
            elif by_scalar:
                out = grouped[:].rearrange("q (u e j) t -> q u e j t", u=2, e=2)
                columns = rows[:].rearrange("q t (u j e) -> q u e j t", u=2, e=2)
                for u in range(2):
                    copy(out=out[:, u], in_=columns[:, u])
            else:
                out = grouped[:].rearrange("q (u e k i) t -> q u k t i e", u=2, e=2, i=2)
                columns = rows[:].rearrange("q t (u k i e) -> q u k t i e", u=2, i=2, e=2)
                for u in range(2):
                    copy(out=out[:, u], in_=columns[:, u])
            live["w_grouped", piece] = grouped

        def quantise_weight(piece):
            nc.vector.quantize_mx(
                out=w_words[:, piece, :].bitcast(FP8X4),
                scales=w_scales[:, piece, :],
                in_=live["w_grouped", piece][:].rearrange("q n t -> q (n t)"),
            )

        def out_of_psum(number):
            return nc.scalar.copy if number == 0 else nc.vector.tensor_copy

        def turn_x(half):
            pairs = live["x", half][:].bitcast(F32)
            turned = psum.tile([P, X_PASSES, 2, P], F32, name="turned", bufs=2)
            for a in range(X_PASSES):
                for u in range(2):
                    first = (2 * a + u) * P
                    nc.tensor.transpose(turned[:, a, u, :], pairs[:, first : first + P], ident[:])
            grouped = work.tile(
                [P, X_PASSES, P, PACK], BF16, name="x_grouped", align_bytes=64, bufs=1
            )
            out_of_psum(half)(
                out=grouped[:].bitcast(F32), in_=turned[:].rearrange("q a u b -> q a b u")
            )
            live["x_grouped", half] = grouped

        def quantise_x(half):
            for a in range(X_PASSES):
                for c in range(GROUP):
                    cols = slice(c * P, (c + 1) * P)
                    nc.vector.quantize_mx(
                        out=x_words[:, half, a, cols].bitcast(FP8X4),
                        scales=x_scales[:, half, a, cols],
                        in_=live["x_grouped", half][:, a, :, :].rearrange("q b t -> q (b t)"),
                    )

        def x_operand(half, a, columns=ROWS):
            return x_words[:, half, a, 0:columns], x_scales[:, half, a, 0:columns]

        def gate_terms(half):
            acc = psum.tile([P, WIDTH], F32, name="turned", bufs=2)
            for a in range(X_PASSES):
                mx(acc[:], x_operand(half, a, P), weight(W_XF + a), a == 0, a == X_PASSES - 1)
            nc.vector.tensor_add(out=gate_add[:, half, :], in0=acc[:], in1=bias_f[:])

        def turn(w):
            g, quarter = divmod(w, 4)
            kind = "h" if quarter < 2 else "p"
            first = 2 * (quarter % 2)
            pairs = live[kind, g][:].bitcast(F32)
            turned = psum.tile([P, 2, 2, P], F32, name="turned", bufs=2)
            for c in range(2):
                for u in range(2):
                    nc.tensor.transpose(
                        turned[:, c, u, :], pairs[:, first + c, u * P : (u + 1) * P], ident[:]
                    )
            live["turned", w] = turned

        def regroup(w):
            g, quarter = divmod(w, 4)
            kind = "h" if quarter < 2 else "p"
            first = 2 * (quarter % 2)
            if first == 0:
                live[kind + "_grouped", g] = work.tile(
                    [P, GROUP, P, PACK], BF16, name=kind + "_grouped", align_bytes=64
                )
            out_of_psum(g)(
                out=live[kind + "_grouped", g][:].bitcast(F32)[:, first : first + 2, :, :],
                in_=live["turned", w][:].rearrange("q c u b -> q c b u"),
            )

        def quantise(kind, g):
            bufs = MX_BUFS[kind]
            words = work.tile([P, ROWS], U32, name=kind + "_words", align_bytes=64, bufs=bufs)
            scales = work.tile([P, ROWS], U8, name=kind + "_scales", align_bytes=64, bufs=bufs)
            nc.vector.quantize_mx(
                out=words[:].bitcast(FP8X4),
                scales=scales[:],
                in_=live[kind + "_grouped", g][:].rearrange("q c b t -> q (c b t)"),
            )
            live[kind + "_mx", g] = (words, scales)

        def rows_operand(kind, g, first=0, columns=ROWS):
            words, scales = live[kind + "_mx", g]
            return words[:, first : first + columns], scales[:, first : first + columns]

        def gate_across(i, kind, u_piece, x_piece):
            g, t = divmod(i, BLOCKS)
            acc = psum.tile([P, ROWS], F32, name="acc_" + kind)
            mx(acc[:], weight(u_piece, t * P, P), rows_operand("h", g), True, False)
            for a in range(X_PASSES):
                mx(
                    acc[:],
                    weight(x_piece + a, t * P, P),
                    x_operand(g // GROUPS_PER_HALF, a),
                    False,
                    a == X_PASSES - 1,
                )
            live["acc_" + kind, i] = acc

        def prop_across(i):
            g, t = divmod(i, BLOCKS)
            acc = psum.tile([P, ROWS], F32, name="acc_p")
            mx(acc[:], weight(W_G, t * P, P), rows_operand("p", g), True, True)
            live["acc_p", i] = acc

        def bias_of(place, t):
            return bias_col[:, place * BLOCKS + t : place * BLOCKS + t + 1]

        def first_sigmoid(i, kind, place):
            gate = work.tile([P, ROWS], F32, name="gate_" + kind, bufs=ACROSS_BUFS)
            nc.scalar.activation(
                out=gate[:],
                in_=live["acc_" + kind, i][:],
                func=FUNC.Sigmoid,
                bias=bias_of(place, i % BLOCKS),
            )
            live[kind, i] = gate

        def second_sigmoid(i, kind):
            nc.scalar.activation(out=live[kind, i][:], in_=live[kind, i][:], func=FUNC.Sigmoid)

        def prop_sum(i):
            g, t = divmod(i, BLOCKS)
            prop = work.tile([P, ROWS], F32, name="prop", bufs=PROP_BUFS)
            nc.vector.scalar_tensor_tensor(
                out=prop[:],
                in0=live["acc_p", i][:],
                scalar=bias_of(B_G, t),
                in1=live["p_grouped", g][:, :, :, t].rearrange("q c b -> q (c b)"),
                op0=ALU.add,
                op1=ALU.add,
            )
            live["prop", i] = prop

        def prop_times_gate(i):
            engine = nc.vector if i == STEPS - 1 else nc.gpsimd
            engine.tensor_tensor(
                out=live["i", i][:], in0=live["prop", i][:], in1=live["i", i][:], op=ALU.mult
            )

        def back(i, kind):
            g, c = divmod(i, GROUP)
            role = "acc_" if g == GROUPS - 1 and c % 2 else "back_"
            bank = psum.tile([P, BLOCKS, P], F32, name=role + kind)
            for t in range(BLOCKS):
                nc.tensor.transpose(
                    bank[:, t, :], live[kind, g * BLOCKS + t][:, c * P : (c + 1) * P], ident[:]
                )
            live["back_" + kind, i] = bank[:].rearrange("b (u e) j -> b u j e", u=2)

        def as_blocks(tile):
            return tile[:].rearrange("b (u j e) -> b u j e", u=2, e=2)

        def tanh_of_m(i):
            g, c = divmod(i, GROUP)
            tanh_m = work.tile([P, WIDTH], F32, name="tanh_m", bufs=TANH_BUFS)
            nc.scalar.activation(out=tanh_m[:], in_=live["m", g][:, c, :], func=FUNC.Tanh)
            live["tanh", i] = tanh_m

        def forget_product(i):
            g, c = divmod(i, GROUP)
            acc = psum.tile([P, WIDTH], F32, name="acc_f")
            mx(acc[:], rows_operand("h", g, c * P, P), weight(W_UF), True, True)
            live["acc_f", i] = acc

        def forget_sum(i):
            forget = work.tile([P, WIDTH], F32, name="forget", bufs=ALONG_BUFS)
            nc.vector.tensor_add(
                out=forget[:], in0=live["acc_f", i][:], in1=gate_add[:, i // STEPS_PER_HALF, :]
            )
            live["f", i] = forget

        def forget_sigmoid(i):
            nc.scalar.activation(out=live["f", i][:], in_=live["f", i][:], func=FUNC.Sigmoid)

        def forget_times_m(i):
            g, c = divmod(i, GROUP)
            nc.gpsimd.tensor_tensor(
                out=live["f", i][:], in0=live["m", g][:, c, :], in1=live["f", i][:], op=ALU.mult
            )

        def kept_sigmoid(i):
            nc.scalar.activation(
                out=live["f", i][:], in_=live["f", i][:], func=FUNC.Sigmoid, bias=FORGET_BIAS
            )

        def finish(i):
            g, c = divmod(i, GROUP)
            batch, first = where(g)
            slot = first + c
            nc.vector.tensor_tensor(
                out=as_blocks(live["tanh", i]),
                in0=live["back_o", i],
                in1=as_blocks(live["tanh", i]),
                op=ALU.mult,
            )
            nc.sync.dma_start(out=out_1[batch, slot, :], in_=live["tanh", i][:])
            nc.vector.tensor_tensor(
                out=as_blocks(live["f", i]),
                in0=live["back_i", i],
                in1=as_blocks(live["f", i]),
                op=ALU.add,
            )
            nc.sync.dma_start(out=out_0[batch, slot, :], in_=live["f", i][:])

        def spread_biases():
            spread = psum.tile([P, WIDTH], F32, name="acc_f")
            nc.tensor.matmul(
                out=spread[:], lhsT=ones[:], rhs=bias_rows[:, 3, :], start=True, stop=True
            )
            nc.scalar.copy(out=bias_f[:], in_=spread[:])
            bias_pairs = bias_rows[:].bitcast(F32)
            for place, name in ((B_I, "back_i"), (B_O, "back_o"), (B_G, "acc_p")):
                bank = psum.tile([P, BLOCKS, P], F32, name=name)
                for u in range(2):
                    nc.tensor.transpose(
                        bank[:, u, :], bias_pairs[:, place, u * P : (u + 1) * P], ident[:]
                    )
                nc.scalar.copy(out=bias_words[:, place, :], in_=bank[:, 0:2, 0])
            nc.scalar.copy(
                out=bias_col[:], in_=bias_words[:].rearrange("q g u -> q (g u)").bitcast(BF16)
            )

        ones = consts.tile([P, P], BF16, name="ones")
        nc.vector.memset(ones[:], 1.0)
        warm = consts.tile([P, 1], F32, name="warm")
        nc.scalar.activation(out=warm[:], in_=ones[:, 0:1], func=FUNC.Sigmoid)
        bias_rows = work.tile([P, 4, WIDTH], BF16, name="loaded", bufs=LOADED_BUFS)
        nc.vector.memset(bias_rows[:].bitcast(F32), 0.0)
        for j, bias in enumerate((b_ui, b_uo, b_g, b_uf)):
            nc.scalar.dma_start(out=bias_rows[0:1, j, :], in_=bias.unsqueeze(0))
        bias_f = consts.tile([P, WIDTH], F32, name="bias_f")
        bias_words = consts.tile([P, 3, 2], F32, name="bias_words")
        bias_col = consts.tile([P, 3 * BLOCKS], F32, name="bias_col")
        ident = consts.tile([P, P], F32, name="ident")
        make_identity(nc, ident[:])


        for n in range(FIRST_STEP, STEPS + BACK_LAG + 1):
            for piece in of_weight(n, W_LEAD + LOAD_LEAD):
                load_weight(piece)
            for half in of_half(n, X_TURN_LEAD + LOAD_LEAD):
                load_x(half)
            for g in of_group(n, M_LOAD_LEAD):
                load_m(g)
            for g in of_group(n, TURN_LEAD + LOAD_LEAD):
                load_rows("h", h_state, g)
            for g in of_group(n, TURN_LEAD + LOAD_LEAD - 2):
                load_rows("p", mem_att, g)

            for piece in of_weight(n, W_LEAD):
                regroup_weight(piece)
            for piece in of_weight(n, W_LEAD - 1):
                quantise_weight(piece)

            if n >= STEPS:
                for i in of_slot(n, -ALONG_LAG):
                    forget_product(i)
                    forget_sum(i)
            for i in of_slot(n, -BACK_LAG):
                back(i, "o")
                back(i, "i")
            for half in of_half(n, X_TURN_LEAD):
                turn_x(half)
            if n == BIAS_STEP:
                spread_biases()
            for i in of_slot(n, -BACK_LAG):
                finish(i)
            for half in of_half(n, X_QUANTISE_LEAD):
                quantise_x(half)
            for g in of_group(n, TURN_LEAD - 2):
                quantise("h", g)
            for g in of_group(n, TURN_LEAD - 4):
                quantise("p", g)

            for i in of_slot(n, 0):
                gate_across(i, "i", W_UI, W_XI)
                gate_across(i, "o", W_UO, W_XO)
                prop_across(i)
            for half in of_half(n, -ALONG_LAG):
                gate_terms(half)
            if n < STEPS:
                for i in of_slot(n, -ALONG_LAG):
                    forget_product(i)
            for i in of_slot(n, 0):
                first_sigmoid(i, "i", B_I)
                first_sigmoid(i, "o", B_O)
                prop_sum(i)
            if n < STEPS:
                for i in of_slot(n, -ALONG_LAG):
                    forget_sum(i)
            for w in of_slot(n, TURN_LEAD):
                turn(w)
                regroup(w)

            for i in of_slot(n, -ALONG_LAG - 1):
                forget_sigmoid(i)
            for i in of_slot(n, 0):
                second_sigmoid(i, "i")
                second_sigmoid(i, "o")
            for i in of_slot(n, -KEPT_LAG):
                kept_sigmoid(i)
            for i in of_slot(n, TANH_LEAD):
                tanh_of_m(i)
            for i in of_slot(n, -1):
                prop_times_gate(i)
            for i in of_slot(n, -ALONG_LAG - 1):
                forget_times_m(i)
